import numpy as np
import ml_dtypes


def mxq(x, axis, fmt="e4m3"):
    dtype, down = {"e4m3": (ml_dtypes.float8_e4m3fn, 7), "e5m2": (ml_dtypes.float8_e5m2, 14)}[fmt]
    v = np.moveaxis(np.asarray(x, np.float32).astype(ml_dtypes.bfloat16).astype(np.float64), axis, -1)
    blocks = v.reshape(v.shape[:-1] + (-1, 32))
    amax = np.abs(blocks).max(-1, keepdims=True)
    byte = np.maximum(np.where(amax > 0, np.frexp(amax)[1] - 1 + 127, 0) - down, 1)
    scale = np.exp2(byte - 127.0)
    codes = (blocks / scale).astype(np.float32).astype(dtype).astype(np.float64)
    return np.moveaxis((codes * scale).reshape(v.shape), -1, axis)


WIDE = False


def mx_kscale(k):
    if not WIDE:
        return np.ones(k)
    levels = np.array([10, -10, 5, -5, 0])
    if k % 512:
        return np.exp2(np.random.permutation(np.resize(levels, k // 32))).repeat(32)
    a = np.empty((k // 512, 16))
    for p in range(k // 512):
        a[p, :8] = np.random.permutation(np.resize(levels, 8))
        for g in range(8):
            far = levels[np.abs(levels - a[p, g]) >= 10]
            a[p, g + 8] = far[np.random.randint(len(far))]
    return np.exp2(a.ravel()).repeat(32)


BF16 = ml_dtypes.bfloat16


def bf(x):
    return np.asarray(x, np.float32).astype(BF16)


def f64(x):
    return np.asarray(x).astype(np.float64)


B, S, HIDDEN, Q_LORA, NUM_HEADS, QK_NOPE, QK_ROPE, KV_LORA = 2, 2048, 1024, 512, 2, 128, 64, 192
QK_HEAD = QK_NOPE + QK_ROPE


def rotate_half(t):
    d = t.shape[-1] // 2
    return np.concatenate([-t[..., d:], t[..., :d]], axis=-1)


def setup_inputs():
    s, t = mx_kscale(HIDDEN), mx_kscale(Q_LORA)
    x = bf(np.random.standard_normal((B, S, HIDDEN)) * s)
    cos = bf(np.random.uniform(size=(B, S, QK_ROPE)))
    sin = bf(np.random.uniform(size=(B, S, QK_ROPE)))
    Wqa = bf(np.random.standard_normal((Q_LORA, HIDDEN)) / np.sqrt(HIDDEN) * t[:, None] / s)
    Wqb = bf(np.random.standard_normal((NUM_HEADS * QK_HEAD, Q_LORA)) / np.sqrt(Q_LORA) / t)
    Wkva = bf(np.random.standard_normal((KV_LORA + QK_ROPE, HIDDEN)) / np.sqrt(HIDDEN) / s)
    return {"x": x, "cos": cos, "sin": sin, "Wqa": Wqa, "Wqb": Wqb, "Wkva": Wkva}


def reference(x, cos, sin, Wqa, Wqb, Wkva):
    b, s, _ = x.shape
    xq = mxq(f64(x), 2, "e4m3")
    qa = xq @ mxq(f64(Wqa), 1, "e4m3").T
    q = (mxq(qa, 2, "e4m3") @ mxq(f64(Wqb), 1, "e4m3").T).reshape(b, s, NUM_HEADS, QK_HEAD)
    q_nope = q[..., :QK_NOPE]
    q_pe = q[..., QK_NOPE:]
    kv = xq @ mxq(f64(Wkva), 1, "e4m3").T
    compressed_kv = kv[..., :KV_LORA]
    k_pe = kv[..., KV_LORA:].reshape(b, s, 1, QK_ROPE)
    c = f64(cos)[:, :, None, :]
    sn = f64(sin)[:, :, None, :]
    q_pe_rot = q_pe * c + rotate_half(q_pe) * sn
    k_pe_rot = k_pe * c + rotate_half(k_pe) * sn
    q_out = np.concatenate([q_nope, q_pe_rot], axis=-1).reshape(b, s, -1)
    k_out = k_pe_rot.reshape(b, s, QK_ROPE)
    return np.concatenate([q_out, k_out, compressed_kv], axis=-1)

@@ -1,0 +1,633 @@
+from contextlib import ExitStack
+
+import concourse.mybir as mybir
+from concourse.masks import make_identity
+
+F32 = mybir.dt.float32
+BF16 = mybir.dt.bfloat16
+U32 = mybir.dt.uint32
+U8 = mybir.dt.uint8
+FP8X4 = mybir.dt.float8_e4m3fn_x4
+MULT = mybir.AluOpType.mult
+ADD = mybir.AluOpType.add
+SUB = mybir.AluOpType.subtract
+
+P = 128
+TOKENS = 4096
+HIDDEN = 1024
+Q_LORA = 512
+ROUNDS = 8
+TILES = 4
+OUT_W = 640
+
+FLOPS = 2 * TOKENS * (HIDDEN * 768 + Q_LORA * 384)
+
+
+def tile_mlaselfattn_t_kernel(tc, x, cos, sin, Wqa, Wqb, Wkva, out):
+    nc = tc.nc
+    with ExitStack() as ctx:
+        ctx.enter_context(tc.manual_schedule())
+        const = ctx.enter_context(tc.tile_pool(name="const", bufs=1))
+        xpool = ctx.enter_context(tc.tile_pool(name="xpool", bufs=ROUNDS))
+        xgp = ctx.enter_context(tc.tile_pool(name="xgp", bufs=6))
+        xcp = ctx.enter_context(tc.tile_pool(name="xcp", bufs=6))
+        qgp = ctx.enter_context(tc.tile_pool(name="qgp", bufs=4))
+        qcp = ctx.enter_context(tc.tile_pool(name="qcp", bufs=10))
+        outp = ctx.enter_context(tc.tile_pool(name="outp", bufs=4))
+        tmpp = ctx.enter_context(tc.tile_pool(name="tmpp", bufs=3))
+        psum = ctx.enter_context(tc.psum_pool(name="psum", bufs=8))
+
+        xv = x.flatten_outer_dims().rearrange("(p r i) k -> p r (i k)", p=P, r=ROUNDS, i=TILES)
+        ov = out.flatten_outer_dims().rearrange("(p r i) c -> p r i c", p=P, r=ROUNDS, i=TILES)
+        cosv = cos.flatten_outer_dims().rearrange("(p t) c -> p t c", p=P)
+        sinv = sin.flatten_outer_dims().rearrange("(p t) c -> p t c", p=P)
+        wqa_v = Wqa.rearrange("(p j) k -> p j k", p=P, j=4)
+
+        wqa_raw = const.tile([P, 4, HIDDEN], BF16, name="wqa_raw", tag="wqa_raw")
+        wkv_raw = const.tile([P, 2, HIDDEN], BF16, name="wkv_raw", tag="wkv_raw")
+        wqb_raw = const.tile([P, 3, Q_LORA], BF16, name="wqb_raw", tag="wqb_raw")
+        cos_sb = const.tile([P, 32, 64], BF16, name="cos_sb", tag="cos_sb")
+        sin_sb = const.tile([P, 32, 64], BF16, name="sin_sb", tag="sin_sb")
+        sinx_sb = const.tile([P, 32, 64], BF16, name="sinx_sb", tag="sinx_sb")
+        ident = const.tile([P, P], F32, name="ident", tag="ident")
+        x_sb = [xpool.tile([P, TILES, HIDDEN], BF16, name="x%d" % r, tag="x") for r in range(ROUNDS)]
+
+        warm_sb = const.tile([P, 512], BF16, name="warm_sb", tag="warm_sb")
+        nc.vector.memset(warm_sb[:], 0.0)
+        make_identity(nc, ident[:])
+
+        def part(ab_):
+            return slice(0, 8) if ab_ == "A" else slice(8, 32)
+
+        def load(what):
+            if what[0:3] == "wqa":
+                j = int(what[3:])
+                nc.sync.dma_start(out=wqa_raw[:, j, :], in_=wqa_v[:, j, :])
+            elif what[0:3] == "x0t":
+                i = int(what[3:])
+                nc.sync.dma_start(out=x_sb[0][:, i, :], in_=xv[:, 0, i * HIDDEN : (i + 1) * HIDDEN])
+            elif what == "wkv":
+                nc.sync.dma_start(out=wkv_raw[:], in_=Wkva.rearrange("(b p) k -> p b k", p=P))
+            elif what == "wqb":
+                nc.sync.dma_start(out=wqb_raw[:, 0:2, :], in_=Wqb.rearrange("(h r) k -> r h k", h=2)[0:128, :, :])
+                nc.sync.dma_start(out=wqb_raw[0:64, 2, :], in_=Wqb[128:192, :])
+                nc.sync.dma_start(out=wqb_raw[64:128, 2, :], in_=Wqb[320:384, :])
+            elif what[0:3] == "cos":
+                nc.sync.dma_start(out=cos_sb[:, part(what[3]), :], in_=cosv[:, part(what[3]), :])
+            elif what[0:3] == "sin":
+                nc.sync.dma_start(out=sin_sb[:, part(what[3]), :], in_=sinv[:, part(what[3]), :])
+            else:
+                r = int(what[1:])
+                nc.sync.dma_start(out=x_sb[r][:].rearrange("p i k -> p (i k)"), in_=xv[:, r, :])
+
+        def new_bank(nm):
+            return psum.tile([P, 512], F32, name=nm, tag="bank")
+
+        warm_bank = {}
+
+        def warm(n):
+            if 0 not in warm_bank:
+                warm_bank[0] = new_bank("warm")
+            for d in range(n):
+                nc.tensor.matmul(out=warm_bank[0][:], lhsT=warm_sb[:, 0:P], rhs=warm_sb[:], start=True, stop=True)
+
+        def transpose_bank(nm, blocks, g):
+            n = len(blocks) * P
+            bank = new_bank(nm)
+            for u in range(2):
+                for b in range(len(blocks)):
+                    nc.tensor.transpose(
+                        out=bank[:, u * n + b * P : u * n + (b + 1) * P],
+                        in_=blocks[b].bitcast(F32)[:, 256 * g + u : 256 * (g + 1) : 2],
+                        identity=ident[:],
+                    )
+            return bank[:, 0 : 2 * n].rearrange("p (u n) -> p n u", u=2)
+
+        def copy_out(eng, dst, src):
+            if eng == "S":
+                nc.scalar.copy(out=dst, in_=src)
+            else:
+                nc.vector.tensor_copy(out=dst, in_=src)
+
+        def drain_words(eng, grouped2d, src):
+            copy_out(eng, grouped2d.bitcast(F32).rearrange("p (n u) -> p n u", u=2), src)
+
+        def transpose_rows(nm, block):
+            bank = new_bank(nm)
+            for w in range(4):
+                nc.tensor.transpose(
+                    out=bank[:, w * P : (w + 1) * P], in_=block.bitcast(F32)[:, 256 * (w // 2) + w % 2 : 256 * (w // 2 + 1) : 2], identity=ident[:]
+                )
+            return bank[:].rearrange("p (g u n) -> p g n u", g=2, u=2)
+
+        def drain_rows(eng, grouped2d, src):
+            copy_out(eng, grouped2d.bitcast(F32).rearrange("p (g n u) -> p g n u", g=2, u=2), src)
+
+        def quant(codes, scales, grouped2d):
+            nc.vector.quantize_mx(out=codes.bitcast(FP8X4), scales=scales, in_=grouped2d)
+
+        def mx(o, l, ls, r_, rs, start, stop):
+            nc.tensor.matmul_mx(
+                out=o, lhsT=l.bitcast(FP8X4), lhsT_scale=ls, rhs=r_.bitcast(FP8X4), rhs_scale=rs,
+                start=start, stop=stop,
+            )
+
+        wqa_g = const.tile([P, 4, 2, P, 4], BF16, name="wqa_g", tag="wqa_g", align_bytes=64)
+        wqa_c = const.tile([P, 4, 2, P], U32, name="wqa_c", tag="wqa_c", align_bytes=64)
+        wqa_s = const.tile([P, 4, 2, P], U8, name="wqa_s", tag="wqa_s", align_bytes=64)
+        wkv_g = const.tile([P, 2, 256, 4], BF16, name="wkv_g", tag="wkv_g", align_bytes=64)
+        wkv_c = const.tile([P, 2, 256], U32, name="wkv_c", tag="wkv_c", align_bytes=64)
+        wkv_s = const.tile([P, 2, 256], U8, name="wkv_s", tag="wkv_s", align_bytes=64)
+        wqb_g = const.tile([P, 384, 4], BF16, name="wqb_g", tag="wqb_g", align_bytes=64)
+        wqb_c = const.tile([P, 384], U32, name="wqb_c", tag="wqb_c", align_bytes=64)
+        wqb_s = const.tile([P, 384], U8, name="wqb_s", tag="wqb_s", align_bytes=64)
+
+        def wqa_t(j, eng):
+            src = transpose_rows("wa%d" % j, wqa_raw[:, j, :])
+            drain_rows(eng, wqa_g[:, j, :, :, :].rearrange("p g n t -> p (g n t)"), src)
+
+        def wqa_q(j):
+            quant(
+                wqa_c[:, j, :, :].rearrange("p g n -> p (g n)"),
+                wqa_s[:, j, :, :].rearrange("p g n -> p (g n)"),
+                wqa_g[:, j, :, :, :].rearrange("p g n t -> p (g n t)"),
+            )
+
+        def wkv_t(g, eng):
+            src = transpose_bank("wk%d" % g, [wkv_raw[:, 0, :], wkv_raw[:, 1, :]], g)
+            drain_words(eng, wkv_g[:, g, :, :].rearrange("p n t -> p (n t)"), src)
+
+        def wkv_q():
+            quant(
+                wkv_c[:].rearrange("p g n -> p (g n)"),
+                wkv_s[:].rearrange("p g n -> p (g n)"),
+                wkv_g[:].rearrange("p g n t -> p (g n t)"),
+            )
+
+        def wqb_t(b, eng):
+            if b == 0:
+                src = transpose_bank("wb0", [wqb_raw[:, 0, :], wqb_raw[:, 1, :]], 0)
+                drain_words(eng, wqb_g[:, 0:256, :].rearrange("p n t -> p (n t)"), src)
+            else:
+                src = transpose_bank("wb1", [wqb_raw[:, 2, :]], 0)
+                drain_words(eng, wqb_g[:, 256:384, :].rearrange("p n t -> p (n t)"), src)
+
+        def wqb_q(b):
+            c = slice(0, 256) if b == 0 else slice(256, 384)
+            quant(wqb_c[:, c], wqb_s[:, c], wqb_g[:, c, :].rearrange("p n t -> p (n t)"))
+
+        def sinx(ab_):
+            nc.vector.tensor_copy(out=sinx_sb[:, part(ab_), 0:32], in_=sin_sb[:, part(ab_), 32:64])
+            nc.vector.tensor_copy(out=sinx_sb[:, part(ab_), 32:64], in_=sin_sb[:, part(ab_), 0:32])
+
+        xg = {}
+        xsrc = {}
+        xc = {}
+        xs = {}
+        qbank = {}
+        qg = {}
+        qc = {}
+        qs = {}
+        kbank = {}
+        nbank = {}
+        pbank = {}
+        osb = {}
+        tk = {}
+        tq = {}
+
+        def xdst(r, i):
+            return xg[(r, i // 2)][:, i % 2, :, :, :].rearrange("p g n t -> p (g n t)")
+
+        def tx(r, i, eng):
+            if (r, i // 2) not in xg:
+                xg[(r, i // 2)] = xgp.tile([P, 2, 2, P, 4], BF16, name="xg%d_%d" % (r, i // 2), tag="xg", align_bytes=64)
+            xsrc[(r, i)] = transpose_rows("xt%d_%d" % (r, i), x_sb[r][:, i, :])
+            if eng == "S":
+                drain_rows("S", xdst(r, i), xsrc[(r, i)])
+
+        def vx(r, i):
+            drain_rows("V", xdst(r, i), xsrc[(r, i)])
+
+        def new_codes(r, pr):
+            if (r, pr) not in xc:
+                xc[(r, pr)] = xcp.tile([P, 2, 2, P], U32, name="xc%d_%d" % (r, pr), tag="xc", align_bytes=64)
+                xs[(r, pr)] = xcp.tile([P, 2, 2, P], U8, name="xs%d_%d" % (r, pr), tag="xs", align_bytes=64)
+
+        def vqx(r, pr):
+            new_codes(r, pr)
+            quant(
+                xc[(r, pr)][:].rearrange("p i g n -> p (i g n)"),
+                xs[(r, pr)][:].rearrange("p i g n -> p (i g n)"),
+                xg[(r, pr)][:].rearrange("p i g n t -> p (i g n t)"),
+            )
+
+        def vqt(r, i):
+            new_codes(r, i // 2)
+            quant(
+                xc[(r, i // 2)][:, i % 2, :, :].rearrange("p g n -> p (g n)"),
+                xs[(r, i // 2)][:, i % 2, :, :].rearrange("p g n -> p (g n)"),
+                xdst(r, i),
+            )
+
+        def a(r, i):
+            pr, i2 = i // 2, i % 2
+            bank = new_bank("qa%d_%d" % (r, i))
+            qbank[(r, i)] = bank
+            for j in range(4):
+                for g in range(2):
+                    mx(
+                        bank[:, j * P : (j + 1) * P],
+                        wqa_c[:, j, g, :], wqa_s[:, j, g, :],
+                        xc[(r, pr)][:, i2, g, :], xs[(r, pr)][:, i2, g, :],
+                        g == 0, g == 1,
+                    )
+
+        def sa(r, i):
+            qg[(r, i)] = qgp.tile([P, P, 4], BF16, name="qg%d_%d" % (r, i), tag="qg", align_bytes=64)
+            nc.scalar.copy(out=qg[(r, i)][:], in_=qbank[(r, i)][:].rearrange("p (j n) -> p n j", j=4))
+
+        def vqa(r, i):
+            qc[(r, i)] = qcp.tile([P, P], U32, name="qc%d_%d" % (r, i), tag="qc", align_bytes=64)
+            qs[(r, i)] = qcp.tile([P, P], U8, name="qs%d_%d" % (r, i), tag="qs", align_bytes=64)
+            quant(qc[(r, i)][:], qs[(r, i)][:], qg[(r, i)][:].rearrange("p n t -> p (n t)"))
+
+        def k(r, pr):
+            bank = new_bank("kv%d_%d" % (r, pr))
+            kbank[(r, pr)] = bank
+            for i2 in range(2):
+                for g in range(2):
+                    mx(
+                        bank[:, i2 * 256 : (i2 + 1) * 256],
+                        xc[(r, pr)][:, i2, g, :], xs[(r, pr)][:, i2, g, :],
+                        wkv_c[:, g, :], wkv_s[:, g, :],
+                        g == 0, g == 1,
+                    )
+
+        def q_pass(r, i, nb, ncol, pb, pcol):
+            mx(nb[:, ncol : ncol + 256], qc[(r, i)][:], qs[(r, i)][:], wqb_c[:, 0:256], wqb_s[:, 0:256], True, True)
+            mx(pb[:, pcol : pcol + P], qc[(r, i)][:], qs[(r, i)][:], wqb_c[:, 256:384], wqb_s[:, 256:384], True, True)
+
+        def q(r):
+            for pr in range(2):
+                nbank[(r, pr)] = new_bank("qn%d_%d" % (r, pr))
+                if pr == 0:
+                    pbank[(r, 0)] = new_bank("qp%d" % r)
+                for i2 in range(2):
+                    i = 2 * pr + i2
+                    q_pass(r, i, nbank[(r, pr)], i2 * 256, pbank[(r, 0)], i * P)
+
+        def qpair(r, pr):
+            nbank[(r, pr)] = new_bank("qn%d_%d" % (r, pr))
+            pbank[(r, 2 * pr)] = new_bank("qp%d_%d" % (r, pr))
+            for i2 in range(2):
+                q_pass(r, 2 * pr + i2, nbank[(r, pr)], i2 * 256, pbank[(r, 2 * pr)], i2 * P)
+
+        def get_o(r):
+            if r not in osb:
+                osb[r] = outp.tile([P, TILES, OUT_W], F32, name="o%d" % r, tag="o")
+            return osb[r]
+
+        def vk(r, pr):
+            if r not in tk:
+                tk[r] = tmpp.tile([P, TILES, 64], F32, name="tk%d" % r, tag="tk")
+            kv = kbank[(r, pr)][:].rearrange("p (i c) -> p i c", i=2)
+            o = get_o(r)
+            t0 = TILES * r + 2 * pr
+            rows = slice(2 * pr, 2 * pr + 2)
+            nc.vector.tensor_tensor(out=o[:, rows, 384:448], in0=kv[:, :, 192:256], in1=cos_sb[:, t0 : t0 + 2, :], op=MULT)
+            nc.vector.tensor_tensor(out=tk[r][:, rows, :], in0=kv[:, :, 192:256], in1=sinx_sb[:, t0 : t0 + 2, :], op=MULT)
+            nc.vector.tensor_copy(out=o[:, rows, 448:640], in_=kv[:, :, 0:192])
+
+        def sn(r, pr):
+            o = get_o(r)[:, 2 * pr : 2 * pr + 2, 0:384].rearrange("p i (h c) -> p i h c", h=2)
+            nc.scalar.copy(out=o[:, :, :, 0:128], in_=nbank[(r, pr)][:].rearrange("p (i h c) -> p i h c", i=2, h=2))
+
+        def ab(r, i0, n):
+            if r not in tq:
+                tq[r] = tmpp.tile([P, TILES, 2, 64], F32, name="tq%d" % r, tag="tq")
+            oq = get_o(r)[:, i0 : i0 + n, 0:384].rearrange("p i (h c) -> p i h c", h=2)
+            pe = pbank[(r, i0)][:, 0 : n * P].rearrange("p (i h c) -> p i h c", i=n, h=2)
+            t0 = TILES * r + i0
+            cb = cos_sb[:, t0 : t0 + n, :].unsqueeze(2).to_broadcast([P, n, 2, 64])
+            sb = sinx_sb[:, t0 : t0 + n, :].unsqueeze(2).to_broadcast([P, n, 2, 64])
+            nc.vector.tensor_tensor(out=oq[:, :, :, 128:192], in0=pe, in1=cb, op=MULT)
+            nc.vector.tensor_tensor(out=tq[r][:, i0 : i0 + n, :, :], in0=pe, in1=sb, op=MULT)
+
+        def engine(e):
+            return nc.gpsimd if e == "G" else nc.vector
+
+        def ck_rows(r, rows, e):
+            o = osb[r]
+            engine(e).tensor_tensor(out=o[:, rows, 384:416], in0=o[:, rows, 384:416], in1=tk[r][:, rows, 32:64], op=SUB)
+            engine(e).tensor_tensor(out=o[:, rows, 416:448], in0=o[:, rows, 416:448], in1=tk[r][:, rows, 0:32], op=ADD)
+
+        def ck(r, e):
+            ck_rows(r, slice(0, TILES), e)
+
+        def ckp(r, pr, e):
+            ck_rows(r, slice(2 * pr, 2 * pr + 2), e)
+
+        def cq(r, i0, n, e):
+            oq = osb[r][:, i0 : i0 + n, 0:384].rearrange("p i (h c) -> p i h c", h=2)
+            t = tq[r][:, i0 : i0 + n, :, :]
+            engine(e).tensor_tensor(out=oq[:, :, :, 128:160], in0=oq[:, :, :, 128:160], in1=t[:, :, :, 32:64], op=SUB)
+            engine(e).tensor_tensor(out=oq[:, :, :, 160:192], in0=oq[:, :, :, 160:192], in1=t[:, :, :, 0:32], op=ADD)
+
+        def store(r, prs, parts):
+            i0 = 2 * prs[0]
+            n = 2 * len(prs)
+            c0 = 0 if "q" in parts else 384
+            c1 = OUT_W if "kv" in parts else 384
+            nc.sync.dma_start(out=ov[:, r, i0 : i0 + n, c0:c1], in_=osb[r][:, i0 : i0 + n, c0:c1])
+
+        load("wqa0")
+        load("wqa1")
+        load("wqa2")
+        load("wqa3")
+        load("x0t0")
+        load("x0t1")
+        load("x0t2")
+        load("x0t3")
+        load("wkv")
+        load("wqb")
+        load("sinA")
+        load("cosA")
+        load("x1")
+        load("x2")
+        load("x3")
+        load("sinB")
+        load("cosB")
+        load("x4")
+        load("x5")
+        load("x6")
+        load("x7")
+        warm(8)
+        wqa_t(0, "S")
+        wqa_q(0)
+        wqa_t(1, "V")
+        warm(1)
+        wqa_q(1)
+        wqa_t(2, "S")
+        wqa_q(2)
+        wqa_t(3, "V")
+        warm(1)
+        wqa_q(3)
+        tx(0, 0, "S")
+        vqt(0, 0)
+        tx(0, 1, "later")
+        warm(1)
+        vx(0, 1)
+        vqt(0, 1)
+        tx(0, 2, "S")
+        vqt(0, 2)
+        tx(0, 3, "later")
+        warm(1)
+        vx(0, 3)
+        vqt(0, 3)
+        wkv_t(0, "S")
+        wkv_t(1, "V")
+        warm(1)
+        wqb_t(0, "S")
+        wqb_t(1, "V")
+        warm(1)
+        wkv_q()
+        wqb_q(0)
+        wqb_q(1)
+        a(0, 0)
+        sa(0, 0)
+        vqa(0, 0)
+        a(0, 1)
+        sa(0, 1)
+        vqa(0, 1)
+        a(0, 2)
+        sa(0, 2)
+        vqa(0, 2)
+        sinx("A")
+        a(0, 3)
+        sa(0, 3)
+        vqa(0, 3)
+        tx(1, 0, "S")
+        tx(1, 1, "S")
+        tx(1, 2, "S")
+        tx(1, 3, "S")
+        k(0, 0)
+        k(0, 1)
+        vk(0, 0)
+        vqx(1, 0)
+        vk(0, 1)
+        vqx(1, 1)
+        tx(2, 0, "S")
+        tx(2, 1, "S")
+        tx(2, 2, "S")
+        tx(2, 3, "S")
+        q(0)
+        sn(0, 0)
+        sn(0, 1)
+        k(1, 0)
+        a(1, 0)
+        k(1, 1)
+        ab(0, 0, 4)
+        vk(1, 0)
+        ck(0, "G")
+        cq(0, 0, 4, "G")
+        vk(1, 1)
+        store(0, [0, 1], ["q", "kv"])
+        sa(1, 0)
+        vqa(1, 0)
+        a(1, 1)
+        sa(1, 1)
+        vqa(1, 1)
+        vqx(2, 0)
+        a(1, 2)
+        sa(1, 2)
+        vqa(1, 2)
+        a(1, 3)
+        sa(1, 3)
+        vqa(1, 3)
+        sinx("B")
+        vqx(2, 1)
+        tx(3, 0, "S")
+        tx(3, 1, "S")
+        tx(3, 2, "S")
+        tx(3, 3, "S")
+        q(1)
+        sn(1, 0)
+        sn(1, 1)
+        k(2, 0)
+        a(2, 0)
+        k(2, 1)
+        ab(1, 0, 4)
+        vk(2, 0)
+        ck(1, "G")
+        cq(1, 0, 4, "G")
+        vk(2, 1)
+        store(1, [0, 1], ["q", "kv"])
+        sa(2, 0)
+        vqa(2, 0)
+        a(2, 1)
+        sa(2, 1)
+        vqa(2, 1)
+        vqx(3, 0)
+        a(2, 2)
+        sa(2, 2)
+        vqa(2, 2)
+        a(2, 3)
+        sa(2, 3)
+        vqa(2, 3)
+        vqx(3, 1)
+        tx(4, 0, "S")
+        tx(4, 1, "S")
+        tx(4, 2, "S")
+        tx(4, 3, "S")
+        q(2)
+        sn(2, 0)
+        sn(2, 1)
+        k(3, 0)
+        a(3, 0)
+        k(3, 1)
+        ab(2, 0, 4)
+        vk(3, 0)
+        ck(2, "G")
+        cq(2, 0, 4, "G")
+        vk(3, 1)
+        store(2, [0, 1], ["q", "kv"])
+        sa(3, 0)
+        vqa(3, 0)
+        a(3, 1)
+        sa(3, 1)
+        vqa(3, 1)
+        vqx(4, 0)
+        a(3, 2)
+        sa(3, 2)
+        vqa(3, 2)
+        a(3, 3)
+        sa(3, 3)
+        vqa(3, 3)
+        vqx(4, 1)
+        tx(5, 0, "S")
+        tx(5, 1, "S")
+        tx(5, 2, "S")
+        tx(5, 3, "S")
+        q(3)
+        sn(3, 0)
+        sn(3, 1)
+        k(4, 0)
+        a(4, 0)
+        k(4, 1)
+        ab(3, 0, 4)
+        vk(4, 0)
+        ck(3, "G")
+        cq(3, 0, 4, "G")
+        vk(4, 1)
+        store(3, [0, 1], ["q", "kv"])
+        sa(4, 0)
+        vqa(4, 0)
+        a(4, 1)
+        sa(4, 1)
+        vqa(4, 1)
+        vqx(5, 0)
+        a(4, 2)
+        sa(4, 2)
+        vqa(4, 2)
+        a(4, 3)
+        sa(4, 3)
+        vqa(4, 3)
+        vqx(5, 1)
+        tx(6, 0, "S")
+        tx(6, 1, "S")
+        tx(6, 2, "S")
+        tx(6, 3, "S")
+        q(4)
+        sn(4, 0)
+        sn(4, 1)
+        k(5, 0)
+        a(5, 0)
+        k(5, 1)
+        ab(4, 0, 4)
+        vk(5, 0)
+        ck(4, "G")
+        cq(4, 0, 4, "G")
+        vk(5, 1)
+        store(4, [0, 1], ["q", "kv"])
+        sa(5, 0)
+        vqa(5, 0)
+        a(5, 1)
+        sa(5, 1)
+        vqa(5, 1)
+        vqx(6, 0)
+        a(5, 2)
+        sa(5, 2)
+        vqa(5, 2)
+        a(5, 3)
+        sa(5, 3)
+        vqa(5, 3)
+        vqx(6, 1)
+        tx(7, 0, "S")
+        tx(7, 1, "S")
+        tx(7, 2, "S")
+        tx(7, 3, "S")
+        q(5)
+        sn(5, 0)
+        sn(5, 1)
+        k(6, 0)
+        k(6, 1)
+        vqx(7, 0)
+        ab(5, 0, 4)
+        vk(6, 0)
+        ck(5, "G")
+        cq(5, 0, 4, "V")
+        store(5, [0, 1], ["q", "kv"])
+        vqx(7, 1)
+        a(6, 0)
+        sa(6, 0)
+        vqa(6, 0)
+        a(6, 1)
+        sa(6, 1)
+        vk(6, 1)
+        vqa(6, 1)
+        a(6, 2)
+        sa(6, 2)
+        vqa(6, 2)
+        a(6, 3)
+        sa(6, 3)
+        vqa(6, 3)
+        k(7, 0)
+        ck(6, "G")
+        store(6, [0, 1], ["kv"])
+        a(7, 0)
+        sa(7, 0)
+        vk(7, 0)
+        k(7, 1)
+        vqa(7, 0)
+        a(7, 1)
+        sa(7, 1)
+        vk(7, 1)
+        qpair(6, 0)
+        sn(6, 0)
+        ck(7, "G")
+        store(7, [0, 1], ["kv"])
+        a(7, 2)
+        sa(7, 2)
+        ab(6, 0, 2)
+        vqa(7, 1)
+        cq(6, 0, 2, "G")
+        store(6, [0], ["q"])
+        qpair(6, 1)
+        a(7, 3)
+        sa(7, 3)
+        sn(6, 1)
+        ab(6, 2, 2)
+        vqa(7, 2)
+        cq(6, 2, 2, "V")
+        vqa(7, 3)
+        store(6, [1], ["q"])
+        qpair(7, 0)
+        sn(7, 0)
+        ab(7, 0, 2)
+        cq(7, 0, 2, "V")
+        store(7, [0], ["q"])
+        qpair(7, 1)
+        sn(7, 1)
+        ab(7, 2, 2)
+        cq(7, 2, 2, "V")
+        store(7, [1], ["q"])

@@ -50,6 +50,7 @@ def tile_mlaselfattn_t_kernel(tc, x, cos, sin, Wqa, Wqb, Wkva, out):
         sin_sb = const.tile([P, 32, 64], BF16, name="sin_sb", tag="sin_sb")
         sinx_sb = const.tile([P, 32, 64], BF16, name="sinx_sb", tag="sinx_sb")
         ident = const.tile([P, P], F32, name="ident", tag="ident")
+        xdp = ctx.enter_context(tc.tile_pool(name="xdp", bufs=3))
         x_sb = [xpool.tile([P, TILES, HIDDEN], BF16, name="x%d" % r, tag="x") for r in range(ROUNDS)]
 
         warm_sb = const.tile([P, 512], BF16, name="warm_sb", tag="warm_sb")
@@ -111,6 +112,27 @@ def tile_mlaselfattn_t_kernel(tc, x, cos, sin, Wqa, Wqb, Wkva, out):
 
         def drain_words(eng, grouped2d, src):
             copy_out(eng, grouped2d.bitcast(F32).rearrange("p (n u) -> p n u", u=2), src)
+
+        xd = {}
+
+        def dx(r, h):
+            if r not in xd:
+                xd[r] = xdp.tile([P, 2, 2, 2 * 256, 2], BF16, name="xd%d" % r, tag="xd", align_bytes=64)
+            nc.vector.tensor_copy(
+                out=xd[r][:, h, :, :, :],
+                in_=x_sb[r][:, 2 * h : 2 * h + 2, :].rearrange("p i (w u e) -> p u (i w) e", u=2, e=2),
+            )
+
+        def transpose_dx(nm, r, i):
+            bank = new_bank(nm)
+            words = xd[r][:, i // 2, :, :, :].rearrange("p u w e -> p (u w e)").bitcast(F32)
+            for g in range(2):
+                for u in range(2):
+                    w0 = 512 * u + 256 * (i % 2) + 128 * g
+                    nc.tensor.transpose(
+                        out=bank[:, (2 * g + u) * P : (2 * g + u + 1) * P], in_=words[:, w0 : w0 + P], identity=ident[:]
+                    )
+            return bank[:].rearrange("p (g u n) -> p g n u", g=2, u=2)
 
         def transpose_rows(nm, block):
             bank = new_bank(nm)
@@ -201,7 +223,10 @@ def tile_mlaselfattn_t_kernel(tc, x, cos, sin, Wqa, Wqb, Wkva, out):
         def tx(r, i, eng):
             if (r, i // 2) not in xg:
                 xg[(r, i // 2)] = xgp.tile([P, 2, 2, P, 4], BF16, name="xg%d_%d" % (r, i // 2), tag="xg", align_bytes=64)
-            xsrc[(r, i)] = transpose_rows("xt%d_%d" % (r, i), x_sb[r][:, i, :])
+            if r in xd:
+                xsrc[(r, i)] = transpose_dx("xt%d_%d" % (r, i), r, i)
+            else:
+                xsrc[(r, i)] = transpose_rows("xt%d_%d" % (r, i), x_sb[r][:, i, :])
             if eng == "S":
                 drain_rows("S", xdst(r, i), xsrc[(r, i)])
 
@@ -431,6 +456,8 @@ def tile_mlaselfattn_t_kernel(tc, x, cos, sin, Wqa, Wqb, Wkva, out):
         ck(0, "G")
         cq(0, 0, 4, "G")
         vk(1, 1)
+        dx(3, 0)
+        dx(3, 1)
         store(0, [0, 1], ["q", "kv"])
         sa(1, 0)
         vqa(1, 0)
@@ -456,6 +483,8 @@ def tile_mlaselfattn_t_kernel(tc, x, cos, sin, Wqa, Wqb, Wkva, out):
         k(2, 0)
         a(2, 0)
         k(2, 1)
+        dx(4, 0)
+        dx(4, 1)
         ab(1, 0, 4)
         vk(2, 0)
         ck(1, "G")
@@ -485,6 +514,8 @@ def tile_mlaselfattn_t_kernel(tc, x, cos, sin, Wqa, Wqb, Wkva, out):
         k(3, 0)
         a(3, 0)
         k(3, 1)
+        dx(5, 0)
+        dx(5, 1)
         ab(2, 0, 4)
         vk(3, 0)
         ck(2, "G")
@@ -514,6 +545,8 @@ def tile_mlaselfattn_t_kernel(tc, x, cos, sin, Wqa, Wqb, Wkva, out):
         k(4, 0)
         a(4, 0)
         k(4, 1)
+        dx(6, 0)
+        dx(6, 1)
         ab(3, 0, 4)
         vk(4, 0)
         ck(3, "G")
@@ -543,6 +576,8 @@ def tile_mlaselfattn_t_kernel(tc, x, cos, sin, Wqa, Wqb, Wkva, out):
         k(5, 0)
         a(5, 0)
         k(5, 1)
+        dx(7, 0)
+        dx(7, 1)
         ab(4, 0, 4)
         vk(5, 0)
         ck(4, "G")

@@ -28,16 +28,17 @@ def tile_mlaselfattn_t_kernel(tc, x, cos, sin, Wqa, Wqb, Wkva, out):
     with ExitStack() as ctx:
         ctx.enter_context(tc.manual_schedule())
         const = ctx.enter_context(tc.tile_pool(name="const", bufs=1))
-        xpool = ctx.enter_context(tc.tile_pool(name="xpool", bufs=ROUNDS))
-        xgp = ctx.enter_context(tc.tile_pool(name="xgp", bufs=6))
-        xcp = ctx.enter_context(tc.tile_pool(name="xcp", bufs=6))
-        qgp = ctx.enter_context(tc.tile_pool(name="qgp", bufs=4))
-        qcp = ctx.enter_context(tc.tile_pool(name="qcp", bufs=10))
+        xpool = ctx.enter_context(tc.tile_pool(name="xpool", bufs=6))
+        xdp = ctx.enter_context(tc.tile_pool(name="xdp", bufs=2))
+        xgp = ctx.enter_context(tc.tile_pool(name="xgp", bufs=3))
+        xcp = ctx.enter_context(tc.tile_pool(name="xcp", bufs=3))
+        qgp = ctx.enter_context(tc.tile_pool(name="qgp", bufs=3))
+        qcp = ctx.enter_context(tc.tile_pool(name="qcp", bufs=5))
         outp = ctx.enter_context(tc.tile_pool(name="outp", bufs=4))
-        tmpp = ctx.enter_context(tc.tile_pool(name="tmpp", bufs=3))
+        tmpp = ctx.enter_context(tc.tile_pool(name="tmpp", bufs=2))
         psum = ctx.enter_context(tc.psum_pool(name="psum", bufs=8))
 
-        xv = x.flatten_outer_dims().rearrange("(p r i) k -> p r (i k)", p=P, r=ROUNDS, i=TILES)
+        xv = x.flatten_outer_dims().rearrange("(p r i) k -> p r i k", p=P, r=ROUNDS, i=TILES)
         ov = out.flatten_outer_dims().rearrange("(p r i) c -> p r i c", p=P, r=ROUNDS, i=TILES)
         cosv = cos.flatten_outer_dims().rearrange("(p t) c -> p t c", p=P)
         sinv = sin.flatten_outer_dims().rearrange("(p t) c -> p t c", p=P)
@@ -46,12 +47,10 @@ def tile_mlaselfattn_t_kernel(tc, x, cos, sin, Wqa, Wqb, Wkva, out):
         wqa_raw = const.tile([P, 4, HIDDEN], BF16, name="wqa_raw", tag="wqa_raw")
         wkv_raw = const.tile([P, 2, HIDDEN], BF16, name="wkv_raw", tag="wkv_raw")
         wqb_raw = const.tile([P, 3, Q_LORA], BF16, name="wqb_raw", tag="wqb_raw")
-        cos_sb = const.tile([P, 32, 64], BF16, name="cos_sb", tag="cos_sb")
+        cs = const.tile([P, 2, 32, 64], BF16, name="cs", tag="cs")
         sin_sb = const.tile([P, 32, 64], BF16, name="sin_sb", tag="sin_sb")
-        sinx_sb = const.tile([P, 32, 64], BF16, name="sinx_sb", tag="sinx_sb")
         ident = const.tile([P, P], F32, name="ident", tag="ident")
-        xdp = ctx.enter_context(tc.tile_pool(name="xdp", bufs=3))
-        x_sb = [xpool.tile([P, TILES, HIDDEN], BF16, name="x%d" % r, tag="x") for r in range(ROUNDS)]
+        x_sb = {}
 
         warm_sb = const.tile([P, 512], BF16, name="warm_sb", tag="warm_sb")
         nc.vector.memset(warm_sb[:], 0.0)
@@ -60,13 +59,15 @@ def tile_mlaselfattn_t_kernel(tc, x, cos, sin, Wqa, Wqb, Wkva, out):
         def part(ab_):
             return slice(0, 8) if ab_ == "A" else slice(8, 32)
 
+        def xtile(r):
+            if r not in x_sb:
+                x_sb[r] = xpool.tile([P, TILES, HIDDEN], BF16, name="x%d" % r, tag="x")
+            return x_sb[r]
+
         def load(what):
             if what[0:3] == "wqa":
                 j = int(what[3:])
                 nc.sync.dma_start(out=wqa_raw[:, j, :], in_=wqa_v[:, j, :])
-            elif what[0:3] == "x0t":
-                i = int(what[3:])
-                nc.sync.dma_start(out=x_sb[0][:, i, :], in_=xv[:, 0, i * HIDDEN : (i + 1) * HIDDEN])
             elif what == "wkv":
                 nc.sync.dma_start(out=wkv_raw[:], in_=Wkva.rearrange("(b p) k -> p b k", p=P))
             elif what == "wqb":
@@ -74,12 +75,18 @@ def tile_mlaselfattn_t_kernel(tc, x, cos, sin, Wqa, Wqb, Wkva, out):
                 nc.sync.dma_start(out=wqb_raw[0:64, 2, :], in_=Wqb[128:192, :])
                 nc.sync.dma_start(out=wqb_raw[64:128, 2, :], in_=Wqb[320:384, :])
             elif what[0:3] == "cos":
-                nc.sync.dma_start(out=cos_sb[:, part(what[3]), :], in_=cosv[:, part(what[3]), :])
+                nc.sync.dma_start(out=cs[:, 0, part(what[3]), :], in_=cosv[:, part(what[3]), :])
             elif what[0:3] == "sin":
                 nc.sync.dma_start(out=sin_sb[:, part(what[3]), :], in_=sinv[:, part(what[3]), :])
+            elif len(what) > 2 and what[2] == "t":
+                r, i = int(what[1]), int(what[3])
+                nc.sync.dma_start(out=xtile(r)[:, i, :], in_=xv[:, r, i, :])
+            elif len(what) > 2:
+                r, h = int(what[1]), int(what[3])
+                nc.sync.dma_start(out=xtile(r)[:, 2 * h : 2 * h + 2, :], in_=xv[:, r, 2 * h : 2 * h + 2, :])
             else:
                 r = int(what[1:])
-                nc.sync.dma_start(out=x_sb[r][:].rearrange("p i k -> p (i k)"), in_=xv[:, r, :])
+                nc.sync.dma_start(out=xtile(r)[:], in_=xv[:, r, :, :])
 
         def new_bank(nm):
             return psum.tile([P, 512], F32, name=nm, tag="bank")
@@ -92,58 +99,11 @@ def tile_mlaselfattn_t_kernel(tc, x, cos, sin, Wqa, Wqb, Wkva, out):
             for d in range(n):
                 nc.tensor.matmul(out=warm_bank[0][:], lhsT=warm_sb[:, 0:P], rhs=warm_sb[:], start=True, stop=True)
 
-        def transpose_bank(nm, blocks, g):
-            n = len(blocks) * P
-            bank = new_bank(nm)
-            for u in range(2):
-                for b in range(len(blocks)):
-                    nc.tensor.transpose(
-                        out=bank[:, u * n + b * P : u * n + (b + 1) * P],
-                        in_=blocks[b].bitcast(F32)[:, 256 * g + u : 256 * (g + 1) : 2],
-                        identity=ident[:],
-                    )
-            return bank[:, 0 : 2 * n].rearrange("p (u n) -> p n u", u=2)
-
         def copy_out(eng, dst, src):
             if eng == "S":
                 nc.scalar.copy(out=dst, in_=src)
             else:
                 nc.vector.tensor_copy(out=dst, in_=src)
-
-        def drain_words(eng, grouped2d, src):
-            copy_out(eng, grouped2d.bitcast(F32).rearrange("p (n u) -> p n u", u=2), src)
-
-        xd = {}
-
-        def dx(r, h):
-            if r not in xd:
-                xd[r] = xdp.tile([P, 2, 2, 2 * 256, 2], BF16, name="xd%d" % r, tag="xd", align_bytes=64)
-            nc.vector.tensor_copy(
-                out=xd[r][:, h, :, :, :],
-                in_=x_sb[r][:, 2 * h : 2 * h + 2, :].rearrange("p i (w u e) -> p u (i w) e", u=2, e=2),
-            )
-
-        def transpose_dx(nm, r, i):
-            bank = new_bank(nm)
-            words = xd[r][:, i // 2, :, :, :].rearrange("p u w e -> p (u w e)").bitcast(F32)
-            for g in range(2):
-                for u in range(2):
-                    w0 = 512 * u + 256 * (i % 2) + 128 * g
-                    nc.tensor.transpose(
-                        out=bank[:, (2 * g + u) * P : (2 * g + u + 1) * P], in_=words[:, w0 : w0 + P], identity=ident[:]
-                    )
-            return bank[:].rearrange("p (g u n) -> p g n u", g=2, u=2)
-
-        def transpose_rows(nm, block):
-            bank = new_bank(nm)
-            for w in range(4):
-                nc.tensor.transpose(
-                    out=bank[:, w * P : (w + 1) * P], in_=block.bitcast(F32)[:, 256 * (w // 2) + w % 2 : 256 * (w // 2 + 1) : 2], identity=ident[:]
-                )
-            return bank[:].rearrange("p (g u n) -> p g n u", g=2, u=2)
-
-        def drain_rows(eng, grouped2d, src):
-            copy_out(eng, grouped2d.bitcast(F32).rearrange("p (g n u) -> p g n u", g=2, u=2), src)
 
         def quant(codes, scales, grouped2d):
             nc.vector.quantize_mx(out=codes.bitcast(FP8X4), scales=scales, in_=grouped2d)
@@ -153,6 +113,31 @@ def tile_mlaselfattn_t_kernel(tc, x, cos, sin, Wqa, Wqb, Wkva, out):
                 out=o, lhsT=l.bitcast(FP8X4), lhsT_scale=ls, rhs=r_.bitcast(FP8X4), rhs_scale=rs,
                 start=start, stop=stop,
             )
+
+        def turn(dst, words):
+            nc.tensor.transpose(out=dst, in_=words, identity=ident[:])
+
+        def turn_raw(nm, block):
+            bank = new_bank(nm)
+            w = block.bitcast(F32)
+            for g in range(2):
+                for u in range(2):
+                    turn(bank[:, (2 * g + u) * P : (2 * g + u + 1) * P], w[:, 256 * g + u : 256 * (g + 1) : 2])
+            return bank[:].rearrange("p (g u n) -> p g n u", g=2, u=2)
+
+        def turn_pair(nm, blocks, g):
+            n = len(blocks) * P
+            bank = new_bank(nm)
+            for u in range(2):
+                for b in range(len(blocks)):
+                    turn(bank[:, u * n + b * P : u * n + (b + 1) * P], blocks[b].bitcast(F32)[:, 256 * g + u : 256 * (g + 1) : 2])
+            return bank[:, 0 : 2 * n].rearrange("p (u n) -> p n u", u=2)
+
+        def words2(ap2d):
+            return ap2d.bitcast(F32).rearrange("p (n u) -> p n u", u=2)
+
+        def words3(ap2d):
+            return ap2d.bitcast(F32).rearrange("p (g n u) -> p g n u", g=2, u=2)
 
         wqa_g = const.tile([P, 4, 2, P, 4], BF16, name="wqa_g", tag="wqa_g", align_bytes=64)
         wqa_c = const.tile([P, 4, 2, P], U32, name="wqa_c", tag="wqa_c", align_bytes=64)
@@ -165,19 +150,19 @@ def tile_mlaselfattn_t_kernel(tc, x, cos, sin, Wqa, Wqb, Wkva, out):
         wqb_s = const.tile([P, 384], U8, name="wqb_s", tag="wqb_s", align_bytes=64)
 
         def wqa_t(j, eng):
-            src = transpose_rows("wa%d" % j, wqa_raw[:, j, :])
-            drain_rows(eng, wqa_g[:, j, :, :, :].rearrange("p g n t -> p (g n t)"), src)
+            src = turn_raw("wa%d" % j, wqa_raw[:, j, :])
+            copy_out(eng, words3(wqa_g[:, j, :, :, :].rearrange("p g n t -> p (g n t)")), src)
 
-        def wqa_q(j):
+        def wqa_q(j, n=1):
             quant(
-                wqa_c[:, j, :, :].rearrange("p g n -> p (g n)"),
-                wqa_s[:, j, :, :].rearrange("p g n -> p (g n)"),
-                wqa_g[:, j, :, :, :].rearrange("p g n t -> p (g n t)"),
+                wqa_c[:, j : j + n, :, :].rearrange("p j g n -> p (j g n)"),
+                wqa_s[:, j : j + n, :, :].rearrange("p j g n -> p (j g n)"),
+                wqa_g[:, j : j + n, :, :, :].rearrange("p j g n t -> p (j g n t)"),
             )
 
         def wkv_t(g, eng):
-            src = transpose_bank("wk%d" % g, [wkv_raw[:, 0, :], wkv_raw[:, 1, :]], g)
-            drain_words(eng, wkv_g[:, g, :, :].rearrange("p n t -> p (n t)"), src)
+            src = turn_pair("wk%d" % g, [wkv_raw[:, 0, :], wkv_raw[:, 1, :]], g)
+            copy_out(eng, words2(wkv_g[:, g, :, :].rearrange("p n t -> p (n t)")), src)
 
         def wkv_q():
             quant(
@@ -188,20 +173,21 @@ def tile_mlaselfattn_t_kernel(tc, x, cos, sin, Wqa, Wqb, Wkva, out):
 
         def wqb_t(b, eng):
             if b == 0:
-                src = transpose_bank("wb0", [wqb_raw[:, 0, :], wqb_raw[:, 1, :]], 0)
-                drain_words(eng, wqb_g[:, 0:256, :].rearrange("p n t -> p (n t)"), src)
+                src = turn_pair("wb0", [wqb_raw[:, 0, :], wqb_raw[:, 1, :]], 0)
+                copy_out(eng, words2(wqb_g[:, 0:256, :].rearrange("p n t -> p (n t)")), src)
             else:
-                src = transpose_bank("wb1", [wqb_raw[:, 2, :]], 0)
-                drain_words(eng, wqb_g[:, 256:384, :].rearrange("p n t -> p (n t)"), src)
+                src = turn_pair("wb1", [wqb_raw[:, 2, :]], 0)
+                copy_out(eng, words2(wqb_g[:, 256:384, :].rearrange("p n t -> p (n t)")), src)
 
         def wqb_q(b):
             c = slice(0, 256) if b == 0 else slice(256, 384)
             quant(wqb_c[:, c], wqb_s[:, c], wqb_g[:, c, :].rearrange("p n t -> p (n t)"))
 
         def sinx(ab_):
-            nc.vector.tensor_copy(out=sinx_sb[:, part(ab_), 0:32], in_=sin_sb[:, part(ab_), 32:64])
-            nc.vector.tensor_copy(out=sinx_sb[:, part(ab_), 32:64], in_=sin_sb[:, part(ab_), 0:32])
+            nc.vector.tensor_copy(out=cs[:, 1, part(ab_), 0:32], in_=sin_sb[:, part(ab_), 32:64])
+            nc.vector.tensor_copy(out=cs[:, 1, part(ab_), 32:64], in_=sin_sb[:, part(ab_), 0:32])
 
+        xd = {}
         xg = {}
         xsrc = {}
         xc = {}
@@ -217,45 +203,42 @@ def tile_mlaselfattn_t_kernel(tc, x, cos, sin, Wqa, Wqb, Wkva, out):
         tk = {}
         tq = {}
 
-        def xdst(r, i):
-            return xg[(r, i // 2)][:, i % 2, :, :, :].rearrange("p g n t -> p (g n t)")
-
-        def tx(r, i, eng):
-            if (r, i // 2) not in xg:
-                xg[(r, i // 2)] = xgp.tile([P, 2, 2, P, 4], BF16, name="xg%d_%d" % (r, i // 2), tag="xg", align_bytes=64)
-            if r in xd:
-                xsrc[(r, i)] = transpose_dx("xt%d_%d" % (r, i), r, i)
-            else:
-                xsrc[(r, i)] = transpose_rows("xt%d_%d" % (r, i), x_sb[r][:, i, :])
-            if eng == "S":
-                drain_rows("S", xdst(r, i), xsrc[(r, i)])
-
-        def vx(r, i):
-            drain_rows("V", xdst(r, i), xsrc[(r, i)])
-
-        def new_codes(r, pr):
-            if (r, pr) not in xc:
-                xc[(r, pr)] = xcp.tile([P, 2, 2, P], U32, name="xc%d_%d" % (r, pr), tag="xc", align_bytes=64)
-                xs[(r, pr)] = xcp.tile([P, 2, 2, P], U8, name="xs%d_%d" % (r, pr), tag="xs", align_bytes=64)
-
-        def vqx(r, pr):
-            new_codes(r, pr)
-            quant(
-                xc[(r, pr)][:].rearrange("p i g n -> p (i g n)"),
-                xs[(r, pr)][:].rearrange("p i g n -> p (i g n)"),
-                xg[(r, pr)][:].rearrange("p i g n t -> p (i g n t)"),
+        def dx(r, i0, n):
+            if r not in xd:
+                xd[r] = xdp.tile([P, 2, TILES * 256, 2], BF16, name="xd%d" % r, tag="xd", align_bytes=64)
+            nc.vector.tensor_copy(
+                out=xd[r][:, :, i0 * 256 : (i0 + n) * 256, :],
+                in_=x_sb[r][:, i0 : i0 + n, :].rearrange("p i (w u e) -> p u (i w) e", u=2, e=2),
             )
 
-        def vqt(r, i):
-            new_codes(r, i // 2)
+        def tx(r, i):
+            if r not in xg:
+                xg[r] = xgp.tile([P, TILES, 2, P, 4], BF16, name="xg%d" % r, tag="xg", align_bytes=64)
+            if r in xd:
+                bank = new_bank("xt%d_%d" % (r, i))
+                for g in range(2):
+                    for u in range(2):
+                        w = xd[r][:, u, i * 256 + g * P : i * 256 + (g + 1) * P, :].rearrange("p w e -> p (w e)").bitcast(F32)
+                        turn(bank[:, (2 * g + u) * P : (2 * g + u + 1) * P], w)
+                xsrc[(r, i)] = bank[:].rearrange("p (g u n) -> p g n u", g=2, u=2)
+            else:
+                xsrc[(r, i)] = turn_raw("xt%d_%d" % (r, i), x_sb[r][:, i, :])
+
+        def ex(r, i, eng):
+            copy_out(eng, words3(xg[r][:, i, :, :, :].rearrange("p g n t -> p (g n t)")), xsrc[(r, i)])
+
+        def vqx(r, i0, n):
+            if r not in xc:
+                xc[r] = xcp.tile([P, TILES, 2, P], U32, name="xc%d" % r, tag="xc", align_bytes=64)
+                xs[r] = xcp.tile([P, TILES, 2, P], U8, name="xs%d" % r, tag="xs", align_bytes=64)
+            t = slice(i0, i0 + n)
             quant(
-                xc[(r, i // 2)][:, i % 2, :, :].rearrange("p g n -> p (g n)"),
-                xs[(r, i // 2)][:, i % 2, :, :].rearrange("p g n -> p (g n)"),
-                xdst(r, i),
+                xc[r][:, t, :, :].rearrange("p i g n -> p (i g n)"),
+                xs[r][:, t, :, :].rearrange("p i g n -> p (i g n)"),
+                xg[r][:, t, :, :, :].rearrange("p i g n t -> p (i g n t)"),
             )
 
         def a(r, i):
-            pr, i2 = i // 2, i % 2
             bank = new_bank("qa%d_%d" % (r, i))
             qbank[(r, i)] = bank
             for j in range(4):
@@ -263,18 +246,26 @@ def tile_mlaselfattn_t_kernel(tc, x, cos, sin, Wqa, Wqb, Wkva, out):
                     mx(
                         bank[:, j * P : (j + 1) * P],
                         wqa_c[:, j, g, :], wqa_s[:, j, g, :],
-                        xc[(r, pr)][:, i2, g, :], xs[(r, pr)][:, i2, g, :],
+                        xc[r][:, i, g, :], xs[r][:, i, g, :],
                         g == 0, g == 1,
                     )
 
-        def sa(r, i):
-            qg[(r, i)] = qgp.tile([P, P, 4], BF16, name="qg%d_%d" % (r, i), tag="qg", align_bytes=64)
-            nc.scalar.copy(out=qg[(r, i)][:], in_=qbank[(r, i)][:].rearrange("p (j n) -> p n j", j=4))
+        def ea(r, i, eng):
+            if (r, i // 2) not in qg:
+                qg[(r, i // 2)] = qgp.tile([P, 2, P, 4], BF16, name="qg%d_%d" % (r, i // 2), tag="qg", align_bytes=64)
+            copy_out(eng, qg[(r, i // 2)][:, i % 2, :, :], qbank[(r, i)][:].rearrange("p (j n) -> p n j", j=4))
 
-        def vqa(r, i):
-            qc[(r, i)] = qcp.tile([P, P], U32, name="qc%d_%d" % (r, i), tag="qc", align_bytes=64)
-            qs[(r, i)] = qcp.tile([P, P], U8, name="qs%d_%d" % (r, i), tag="qs", align_bytes=64)
-            quant(qc[(r, i)][:], qs[(r, i)][:], qg[(r, i)][:].rearrange("p n t -> p (n t)"))
+        def vqa(r, i, n):
+            pr = i // 2
+            if (r, pr) not in qc:
+                qc[(r, pr)] = qcp.tile([P, 2, P], U32, name="qc%d_%d" % (r, pr), tag="qc", align_bytes=64)
+                qs[(r, pr)] = qcp.tile([P, 2, P], U8, name="qs%d_%d" % (r, pr), tag="qs", align_bytes=64)
+            t = slice(i % 2, i % 2 + n)
+            quant(
+                qc[(r, pr)][:, t, :].rearrange("p i n -> p (i n)"),
+                qs[(r, pr)][:, t, :].rearrange("p i n -> p (i n)"),
+                qg[(r, pr)][:, t, :, :].rearrange("p i n t -> p (i n t)"),
+            )
 
         def k(r, pr):
             bank = new_bank("kv%d_%d" % (r, pr))
@@ -283,14 +274,15 @@ def tile_mlaselfattn_t_kernel(tc, x, cos, sin, Wqa, Wqb, Wkva, out):
                 for g in range(2):
                     mx(
                         bank[:, i2 * 256 : (i2 + 1) * 256],
-                        xc[(r, pr)][:, i2, g, :], xs[(r, pr)][:, i2, g, :],
+                        xc[r][:, 2 * pr + i2, g, :], xs[r][:, 2 * pr + i2, g, :],
                         wkv_c[:, g, :], wkv_s[:, g, :],
                         g == 0, g == 1,
                     )
 
         def q_pass(r, i, nb, ncol, pb, pcol):
-            mx(nb[:, ncol : ncol + 256], qc[(r, i)][:], qs[(r, i)][:], wqb_c[:, 0:256], wqb_s[:, 0:256], True, True)
-            mx(pb[:, pcol : pcol + P], qc[(r, i)][:], qs[(r, i)][:], wqb_c[:, 256:384], wqb_s[:, 256:384], True, True)
+            l, ls = qc[(r, i // 2)][:, i % 2, :], qs[(r, i // 2)][:, i % 2, :]
+            mx(nb[:, ncol : ncol + 256], l, ls, wqb_c[:, 0:256], wqb_s[:, 0:256], True, True)
+            mx(pb[:, pcol : pcol + P], l, ls, wqb_c[:, 256:384], wqb_s[:, 256:384], True, True)
 
         def q(r):
             for pr in range(2):
@@ -312,16 +304,22 @@ def tile_mlaselfattn_t_kernel(tc, x, cos, sin, Wqa, Wqb, Wkva, out):
                 osb[r] = outp.tile([P, TILES, OUT_W], F32, name="o%d" % r, tag="o")
             return osb[r]
 
+        def kv_view(r, pr):
+            return kbank[(r, pr)][:].rearrange("p (i c) -> p i c", i=2)
+
         def vk(r, pr):
             if r not in tk:
-                tk[r] = tmpp.tile([P, TILES, 64], F32, name="tk%d" % r, tag="tk")
-            kv = kbank[(r, pr)][:].rearrange("p (i c) -> p i c", i=2)
-            o = get_o(r)
+                tk[r] = tmpp.tile([P, TILES, 2, 64], F32, name="tk%d" % r, tag="tk")
             t0 = TILES * r + 2 * pr
-            rows = slice(2 * pr, 2 * pr + 2)
-            nc.vector.tensor_tensor(out=o[:, rows, 384:448], in0=kv[:, :, 192:256], in1=cos_sb[:, t0 : t0 + 2, :], op=MULT)
-            nc.vector.tensor_tensor(out=tk[r][:, rows, :], in0=kv[:, :, 192:256], in1=sinx_sb[:, t0 : t0 + 2, :], op=MULT)
-            nc.vector.tensor_copy(out=o[:, rows, 448:640], in_=kv[:, :, 0:192])
+            nc.vector.tensor_tensor(
+                out=tk[r][:, 2 * pr : 2 * pr + 2, :, :],
+                in0=kv_view(r, pr)[:, :, 192:256].unsqueeze(2).to_broadcast([P, 2, 2, 64]),
+                in1=cs[:, :, t0 : t0 + 2, :].rearrange("p b t c -> p t b c"),
+                op=MULT,
+            )
+
+        def ek(r, pr, eng):
+            copy_out(eng, get_o(r)[:, 2 * pr : 2 * pr + 2, 448:640], kv_view(r, pr)[:, :, 0:192])
 
         def sn(r, pr):
             o = get_o(r)[:, 2 * pr : 2 * pr + 2, 0:384].rearrange("p i (h c) -> p i h c", h=2)
@@ -329,38 +327,35 @@ def tile_mlaselfattn_t_kernel(tc, x, cos, sin, Wqa, Wqb, Wkva, out):
 
         def ab(r, i0, n):
             if r not in tq:
-                tq[r] = tmpp.tile([P, TILES, 2, 64], F32, name="tq%d" % r, tag="tq")
-            oq = get_o(r)[:, i0 : i0 + n, 0:384].rearrange("p i (h c) -> p i h c", h=2)
+                tq[r] = tmpp.tile([P, 2, TILES, 2, 64], F32, name="tq%d" % r, tag="tq")
             pe = pbank[(r, i0)][:, 0 : n * P].rearrange("p (i h c) -> p i h c", i=n, h=2)
             t0 = TILES * r + i0
-            cb = cos_sb[:, t0 : t0 + n, :].unsqueeze(2).to_broadcast([P, n, 2, 64])
-            sb = sinx_sb[:, t0 : t0 + n, :].unsqueeze(2).to_broadcast([P, n, 2, 64])
-            nc.vector.tensor_tensor(out=oq[:, :, :, 128:192], in0=pe, in1=cb, op=MULT)
-            nc.vector.tensor_tensor(out=tq[r][:, i0 : i0 + n, :, :], in0=pe, in1=sb, op=MULT)
+            for b in range(2):
+                nc.vector.tensor_tensor(
+                    out=tq[r][:, b, i0 : i0 + n, :, :],
+                    in0=pe,
+                    in1=cs[:, b, t0 : t0 + n, :].unsqueeze(2).to_broadcast([P, n, 2, 64]),
+                    op=MULT,
+                )
 
         def engine(e):
             return nc.gpsimd if e == "G" else nc.vector
 
-        def ck_rows(r, rows, e):
-            o = osb[r]
-            engine(e).tensor_tensor(out=o[:, rows, 384:416], in0=o[:, rows, 384:416], in1=tk[r][:, rows, 32:64], op=SUB)
-            engine(e).tensor_tensor(out=o[:, rows, 416:448], in0=o[:, rows, 416:448], in1=tk[r][:, rows, 0:32], op=ADD)
-
-        def ck(r, e):
-            ck_rows(r, slice(0, TILES), e)
-
-        def ckp(r, pr, e):
-            ck_rows(r, slice(2 * pr, 2 * pr + 2), e)
+        def ck(r, i0, n, e):
+            o = get_o(r)
+            t = tk[r]
+            i = slice(i0, i0 + n)
+            engine(e).tensor_tensor(out=o[:, i, 384:416], in0=t[:, i, 0, 0:32], in1=t[:, i, 1, 32:64], op=SUB)
+            engine(e).tensor_tensor(out=o[:, i, 416:448], in0=t[:, i, 0, 32:64], in1=t[:, i, 1, 0:32], op=ADD)
 
         def cq(r, i0, n, e):
-            oq = osb[r][:, i0 : i0 + n, 0:384].rearrange("p i (h c) -> p i h c", h=2)
-            t = tq[r][:, i0 : i0 + n, :, :]
-            engine(e).tensor_tensor(out=oq[:, :, :, 128:160], in0=oq[:, :, :, 128:160], in1=t[:, :, :, 32:64], op=SUB)
-            engine(e).tensor_tensor(out=oq[:, :, :, 160:192], in0=oq[:, :, :, 160:192], in1=t[:, :, :, 0:32], op=ADD)
+            oq = get_o(r)[:, i0 : i0 + n, 0:384].rearrange("p i (h c) -> p i h c", h=2)
+            t = tq[r]
+            i = slice(i0, i0 + n)
+            engine(e).tensor_tensor(out=oq[:, :, :, 128:160], in0=t[:, 0, i, :, 0:32], in1=t[:, 1, i, :, 32:64], op=SUB)
+            engine(e).tensor_tensor(out=oq[:, :, :, 160:192], in0=t[:, 0, i, :, 32:64], in1=t[:, 1, i, :, 0:32], op=ADD)
 
-        def store(r, prs, parts):
-            i0 = 2 * prs[0]
-            n = 2 * len(prs)
+        def store(r, i0, n, parts):
             c0 = 0 if "q" in parts else 384
             c1 = OUT_W if "kv" in parts else 384
             nc.sync.dma_start(out=ov[:, r, i0 : i0 + n, c0:c1], in_=osb[r][:, i0 : i0 + n, c0:c1])
@@ -375,17 +370,15 @@ def tile_mlaselfattn_t_kernel(tc, x, cos, sin, Wqa, Wqb, Wkva, out):
         load("x0t3")
         load("wkv")
         load("wqb")
+        load("x1")
         load("sinA")
         load("cosA")
-        load("x1")
         load("x2")
         load("x3")
-        load("sinB")
-        load("cosB")
         load("x4")
         load("x5")
-        load("x6")
-        load("x7")
+        load("sinB")
+        load("cosB")
         warm(8)
         wqa_t(0, "S")
         wqa_q(0)
@@ -397,18 +390,20 @@ def tile_mlaselfattn_t_kernel(tc, x, cos, sin, Wqa, Wqb, Wkva, out):
         wqa_t(3, "V")
         warm(1)
         wqa_q(3)
-        tx(0, 0, "S")
-        vqt(0, 0)
-        tx(0, 1, "later")
+        tx(0, 0)
+        ex(0, 0, "S")
+        vqx(0, 0, 1)
+        tx(0, 1)
         warm(1)
-        vx(0, 1)
-        vqt(0, 1)
-        tx(0, 2, "S")
-        vqt(0, 2)
-        tx(0, 3, "later")
+        ex(0, 1, "V")
+        vqx(0, 1, 1)
+        tx(0, 2)
+        ex(0, 2, "S")
+        vqx(0, 2, 1)
+        tx(0, 3)
         warm(1)
-        vx(0, 3)
-        vqt(0, 3)
+        ex(0, 3, "V")
+        vqx(0, 3, 1)
         wkv_t(0, "S")
         wkv_t(1, "V")
         warm(1)
@@ -419,32 +414,44 @@ def tile_mlaselfattn_t_kernel(tc, x, cos, sin, Wqa, Wqb, Wkva, out):
         wqb_q(0)
         wqb_q(1)
         a(0, 0)
-        sa(0, 0)
-        vqa(0, 0)
+        ea(0, 0, "S")
+        vqa(0, 0, 1)
         a(0, 1)
-        sa(0, 1)
-        vqa(0, 1)
+        ea(0, 1, "S")
+        vqa(0, 1, 1)
         a(0, 2)
-        sa(0, 2)
-        vqa(0, 2)
+        ea(0, 2, "S")
+        vqa(0, 2, 1)
         sinx("A")
         a(0, 3)
-        sa(0, 3)
-        vqa(0, 3)
-        tx(1, 0, "S")
-        tx(1, 1, "S")
-        tx(1, 2, "S")
-        tx(1, 3, "S")
+        ea(0, 3, "S")
+        vqa(0, 3, 1)
+        tx(1, 0)
+        ex(1, 0, "S")
+        tx(1, 1)
+        ex(1, 1, "S")
+        tx(1, 2)
+        ex(1, 2, "S")
+        tx(1, 3)
+        ex(1, 3, "S")
         k(0, 0)
         k(0, 1)
         vk(0, 0)
-        vqx(1, 0)
+        ek(0, 0, "V")
+        vqx(1, 0, 2)
+        load("x6")
         vk(0, 1)
-        vqx(1, 1)
-        tx(2, 0, "S")
-        tx(2, 1, "S")
-        tx(2, 2, "S")
-        tx(2, 3, "S")
+        ek(0, 1, "V")
+        vqx(1, 2, 2)
+        dx(3, 0, 4)
+        tx(2, 0)
+        ex(2, 0, "S")
+        tx(2, 1)
+        ex(2, 1, "S")
+        tx(2, 2)
+        ex(2, 2, "S")
+        tx(2, 3)
+        ex(2, 3, "S")
         q(0)
         sn(0, 0)
         sn(0, 1)
@@ -453,216 +460,233 @@ def tile_mlaselfattn_t_kernel(tc, x, cos, sin, Wqa, Wqb, Wkva, out):
         k(1, 1)
         ab(0, 0, 4)
         vk(1, 0)
-        ck(0, "G")
+        ek(1, 0, "V")
+        ck(0, 0, 4, "G")
         cq(0, 0, 4, "G")
         vk(1, 1)
-        dx(3, 0)
-        dx(3, 1)
-        store(0, [0, 1], ["q", "kv"])
-        sa(1, 0)
-        vqa(1, 0)
+        ek(1, 1, "V")
+        store(0, 0, 4, ["q", "kv"])
+        ea(1, 0, "S")
         a(1, 1)
-        sa(1, 1)
-        vqa(1, 1)
-        vqx(2, 0)
+        ea(1, 1, "S")
+        vqa(1, 0, 2)
+        vqx(2, 0, 2)
         a(1, 2)
-        sa(1, 2)
-        vqa(1, 2)
+        ea(1, 2, "S")
         a(1, 3)
-        sa(1, 3)
-        vqa(1, 3)
+        ea(1, 3, "S")
+        vqa(1, 2, 2)
+        load("x7")
         sinx("B")
-        vqx(2, 1)
-        tx(3, 0, "S")
-        tx(3, 1, "S")
-        tx(3, 2, "S")
-        tx(3, 3, "S")
+        vqx(2, 2, 2)
+        dx(4, 0, 4)
+        tx(3, 0)
+        ex(3, 0, "S")
+        tx(3, 1)
+        ex(3, 1, "S")
+        tx(3, 2)
+        ex(3, 2, "S")
+        tx(3, 3)
+        ex(3, 3, "S")
         q(1)
         sn(1, 0)
         sn(1, 1)
         k(2, 0)
         a(2, 0)
         k(2, 1)
-        dx(4, 0)
-        dx(4, 1)
         ab(1, 0, 4)
         vk(2, 0)
-        ck(1, "G")
+        ek(2, 0, "V")
+        ck(1, 0, 4, "G")
         cq(1, 0, 4, "G")
         vk(2, 1)
-        store(1, [0, 1], ["q", "kv"])
-        sa(2, 0)
-        vqa(2, 0)
+        ek(2, 1, "V")
+        store(1, 0, 4, ["q", "kv"])
+        ea(2, 0, "S")
         a(2, 1)
-        sa(2, 1)
-        vqa(2, 1)
-        vqx(3, 0)
+        ea(2, 1, "S")
+        vqa(2, 0, 2)
+        vqx(3, 0, 2)
         a(2, 2)
-        sa(2, 2)
-        vqa(2, 2)
+        ea(2, 2, "S")
         a(2, 3)
-        sa(2, 3)
-        vqa(2, 3)
-        vqx(3, 1)
-        tx(4, 0, "S")
-        tx(4, 1, "S")
-        tx(4, 2, "S")
-        tx(4, 3, "S")
+        ea(2, 3, "S")
+        vqa(2, 2, 2)
+        vqx(3, 2, 2)
+        dx(5, 0, 4)
+        tx(4, 0)
+        ex(4, 0, "S")
+        tx(4, 1)
+        ex(4, 1, "S")
+        tx(4, 2)
+        ex(4, 2, "S")
+        tx(4, 3)
+        ex(4, 3, "S")
         q(2)
         sn(2, 0)
         sn(2, 1)
         k(3, 0)
         a(3, 0)
         k(3, 1)
-        dx(5, 0)
-        dx(5, 1)
         ab(2, 0, 4)
         vk(3, 0)
-        ck(2, "G")
+        ek(3, 0, "V")
+        ck(2, 0, 4, "G")
         cq(2, 0, 4, "G")
         vk(3, 1)
-        store(2, [0, 1], ["q", "kv"])
-        sa(3, 0)
-        vqa(3, 0)
+        ek(3, 1, "V")
+        store(2, 0, 4, ["q", "kv"])
+        ea(3, 0, "S")
         a(3, 1)
-        sa(3, 1)
-        vqa(3, 1)
-        vqx(4, 0)
+        ea(3, 1, "S")
+        vqa(3, 0, 2)
+        vqx(4, 0, 2)
         a(3, 2)
-        sa(3, 2)
-        vqa(3, 2)
+        ea(3, 2, "S")
         a(3, 3)
-        sa(3, 3)
-        vqa(3, 3)
-        vqx(4, 1)
-        tx(5, 0, "S")
-        tx(5, 1, "S")
-        tx(5, 2, "S")
-        tx(5, 3, "S")
+        ea(3, 3, "S")
+        vqa(3, 2, 2)
+        vqx(4, 2, 2)
+        dx(6, 0, 4)
+        tx(5, 0)
+        ex(5, 0, "S")
+        tx(5, 1)
+        ex(5, 1, "S")
+        tx(5, 2)
+        ex(5, 2, "S")
+        tx(5, 3)
+        ex(5, 3, "S")
         q(3)
         sn(3, 0)
         sn(3, 1)
         k(4, 0)
         a(4, 0)
         k(4, 1)
-        dx(6, 0)
-        dx(6, 1)
         ab(3, 0, 4)
         vk(4, 0)
-        ck(3, "G")
+        ek(4, 0, "V")
+        ck(3, 0, 4, "G")
         cq(3, 0, 4, "G")
         vk(4, 1)
-        store(3, [0, 1], ["q", "kv"])
-        sa(4, 0)
-        vqa(4, 0)
+        ek(4, 1, "V")
+        store(3, 0, 4, ["q", "kv"])
+        ea(4, 0, "S")
         a(4, 1)
-        sa(4, 1)
-        vqa(4, 1)
-        vqx(5, 0)
+        ea(4, 1, "S")
+        vqa(4, 0, 2)
+        vqx(5, 0, 2)
         a(4, 2)
-        sa(4, 2)
-        vqa(4, 2)
+        ea(4, 2, "S")
         a(4, 3)
-        sa(4, 3)
-        vqa(4, 3)
-        vqx(5, 1)
-        tx(6, 0, "S")
-        tx(6, 1, "S")
-        tx(6, 2, "S")
-        tx(6, 3, "S")
+        ea(4, 3, "S")
+        vqa(4, 2, 2)
+        vqx(5, 2, 2)
+        dx(7, 0, 4)
+        tx(6, 0)
+        ex(6, 0, "S")
+        tx(6, 1)
+        ex(6, 1, "S")
+        tx(6, 2)
+        ex(6, 2, "S")
+        tx(6, 3)
+        ex(6, 3, "S")
         q(4)
         sn(4, 0)
         sn(4, 1)
         k(5, 0)
         a(5, 0)
         k(5, 1)
-        dx(7, 0)
-        dx(7, 1)
         ab(4, 0, 4)
         vk(5, 0)
-        ck(4, "G")
+        ek(5, 0, "V")
+        ck(4, 0, 4, "G")
         cq(4, 0, 4, "G")
         vk(5, 1)
-        store(4, [0, 1], ["q", "kv"])
-        sa(5, 0)
-        vqa(5, 0)
+        ek(5, 1, "V")
+        store(4, 0, 4, ["q", "kv"])
+        ea(5, 0, "S")
         a(5, 1)
-        sa(5, 1)
-        vqa(5, 1)
-        vqx(6, 0)
+        ea(5, 1, "S")
+        vqa(5, 0, 2)
+        vqx(6, 0, 2)
         a(5, 2)
-        sa(5, 2)
-        vqa(5, 2)
+        ea(5, 2, "S")
         a(5, 3)
-        sa(5, 3)
-        vqa(5, 3)
-        vqx(6, 1)
-        tx(7, 0, "S")
-        tx(7, 1, "S")
-        tx(7, 2, "S")
-        tx(7, 3, "S")
+        ea(5, 3, "S")
+        vqa(5, 2, 2)
+        vqx(6, 2, 2)
+        tx(7, 0)
+        ex(7, 0, "S")
+        tx(7, 1)
+        ex(7, 1, "S")
+        tx(7, 2)
+        ex(7, 2, "S")
+        tx(7, 3)
+        ex(7, 3, "S")
         q(5)
         sn(5, 0)
         sn(5, 1)
         k(6, 0)
         k(6, 1)
-        vqx(7, 0)
+        vqx(7, 0, 2)
         ab(5, 0, 4)
         vk(6, 0)
-        ck(5, "G")
+        ek(6, 0, "V")
+        ck(5, 0, 4, "G")
         cq(5, 0, 4, "V")
-        store(5, [0, 1], ["q", "kv"])
-        vqx(7, 1)
+        store(5, 0, 4, ["q", "kv"])
+        vqx(7, 2, 2)
         a(6, 0)
-        sa(6, 0)
-        vqa(6, 0)
+        ea(6, 0, "S")
         a(6, 1)
-        sa(6, 1)
+        ea(6, 1, "S")
         vk(6, 1)
-        vqa(6, 1)
+        ek(6, 1, "V")
+        vqa(6, 0, 2)
         a(6, 2)
-        sa(6, 2)
-        vqa(6, 2)
+        ea(6, 2, "S")
         a(6, 3)
-        sa(6, 3)
-        vqa(6, 3)
+        ea(6, 3, "S")
+        vqa(6, 2, 2)
         k(7, 0)
-        ck(6, "G")
-        store(6, [0, 1], ["kv"])
+        ck(6, 0, 4, "G")
+        store(6, 0, 4, ["kv"])
         a(7, 0)
-        sa(7, 0)
+        ea(7, 0, "S")
         vk(7, 0)
+        ek(7, 0, "V")
         k(7, 1)
-        vqa(7, 0)
+        vqa(7, 0, 1)
         a(7, 1)
-        sa(7, 1)
+        ea(7, 1, "S")
         vk(7, 1)
+        ek(7, 1, "V")
         qpair(6, 0)
         sn(6, 0)
-        ck(7, "G")
-        store(7, [0, 1], ["kv"])
+        ck(7, 0, 4, "G")
+        store(7, 0, 4, ["kv"])
         a(7, 2)
-        sa(7, 2)
+        ea(7, 2, "S")
         ab(6, 0, 2)
-        vqa(7, 1)
+        vqa(7, 1, 1)
         cq(6, 0, 2, "G")
-        store(6, [0], ["q"])
+        store(6, 0, 2, ["q"])
         qpair(6, 1)
         a(7, 3)
-        sa(7, 3)
+        ea(7, 3, "S")
         sn(6, 1)
         ab(6, 2, 2)
-        vqa(7, 2)
+        vqa(7, 2, 1)
         cq(6, 2, 2, "V")
-        vqa(7, 3)
-        store(6, [1], ["q"])
+        vqa(7, 3, 1)
+        store(6, 2, 2, ["q"])
         qpair(7, 0)
         sn(7, 0)
         ab(7, 0, 2)
         cq(7, 0, 2, "V")
-        store(7, [0], ["q"])
+        store(7, 0, 2, ["q"])
         qpair(7, 1)
         sn(7, 1)
         ab(7, 2, 2)
         cq(7, 2, 2, "V")
-        store(7, [1], ["q"])
+        store(7, 2, 2, ["q"])

from contextlib import ExitStack

import concourse.mybir as mybir
from concourse.masks import make_identity

F32 = mybir.dt.float32
BF16 = mybir.dt.bfloat16
U32 = mybir.dt.uint32
U8 = mybir.dt.uint8
FP8X4 = mybir.dt.float8_e4m3fn_x4
MULT = mybir.AluOpType.mult
ADD = mybir.AluOpType.add
SUB = mybir.AluOpType.subtract

P = 128
TOKENS = 4096
HIDDEN = 1024
Q_LORA = 512
ROUNDS = 8
TILES = 4
OUT_W = 640

FLOPS = 2 * TOKENS * (HIDDEN * 768 + Q_LORA * 384)


def tile_mlaselfattn_t_kernel(tc, x, cos, sin, Wqa, Wqb, Wkva, out):
    nc = tc.nc
    with ExitStack() as ctx:
        ctx.enter_context(tc.manual_schedule())
        const = ctx.enter_context(tc.tile_pool(name="const", bufs=1))
        xpool = ctx.enter_context(tc.tile_pool(name="xpool", bufs=6))
        xdp = ctx.enter_context(tc.tile_pool(name="xdp", bufs=2))
        xgp = ctx.enter_context(tc.tile_pool(name="xgp", bufs=3))
        xcp = ctx.enter_context(tc.tile_pool(name="xcp", bufs=3))
        qgp = ctx.enter_context(tc.tile_pool(name="qgp", bufs=3))
        qcp = ctx.enter_context(tc.tile_pool(name="qcp", bufs=5))
        outp = ctx.enter_context(tc.tile_pool(name="outp", bufs=4))
        tmpp = ctx.enter_context(tc.tile_pool(name="tmpp", bufs=2))
        psum = ctx.enter_context(tc.psum_pool(name="psum", bufs=8))

        xv = x.flatten_outer_dims().rearrange("(p r i) k -> p r i k", p=P, r=ROUNDS, i=TILES)
        ov = out.flatten_outer_dims().rearrange("(p r i) c -> p r i c", p=P, r=ROUNDS, i=TILES)
        cosv = cos.flatten_outer_dims().rearrange("(p t) c -> p t c", p=P)
        sinv = sin.flatten_outer_dims().rearrange("(p t) c -> p t c", p=P)
        wqa_v = Wqa.rearrange("(p j) k -> p j k", p=P, j=4)

        wqa_raw = const.tile([P, 4, HIDDEN], BF16, name="wqa_raw", tag="wqa_raw")
        wkv_raw = const.tile([P, 2, HIDDEN], BF16, name="wkv_raw", tag="wkv_raw")
        wqb_raw = const.tile([P, 3, Q_LORA], BF16, name="wqb_raw", tag="wqb_raw")
        cs = const.tile([P, 2, 32, 64], BF16, name="cs", tag="cs")
        sin_sb = const.tile([P, 32, 64], BF16, name="sin_sb", tag="sin_sb")
        ident = const.tile([P, P], F32, name="ident", tag="ident")
        x_sb = {}

        warm_sb = const.tile([P, 512], BF16, name="warm_sb", tag="warm_sb")
        nc.vector.memset(warm_sb[:], 0.0)
        make_identity(nc, ident[:])

        def part(ab_):
            return slice(0, 8) if ab_ == "A" else slice(8, 32)

        def xtile(r):
            if r not in x_sb:
                x_sb[r] = xpool.tile([P, TILES, HIDDEN], BF16, name="x%d" % r, tag="x")
            return x_sb[r]

        def load(what):
            if what[0:3] == "wqa":
                j = int(what[3:])
                nc.sync.dma_start(out=wqa_raw[:, j, :], in_=wqa_v[:, j, :])
            elif what == "wkv":
                nc.sync.dma_start(out=wkv_raw[:], in_=Wkva.rearrange("(b p) k -> p b k", p=P))
            elif what == "wqb":
                nc.sync.dma_start(out=wqb_raw[:, 0:2, :], in_=Wqb.rearrange("(h r) k -> r h k", h=2)[0:128, :, :])
                nc.sync.dma_start(out=wqb_raw[0:64, 2, :], in_=Wqb[128:192, :])
                nc.sync.dma_start(out=wqb_raw[64:128, 2, :], in_=Wqb[320:384, :])
            elif what[0:3] == "cos":
                nc.sync.dma_start(out=cs[:, 0, part(what[3]), :], in_=cosv[:, part(what[3]), :])
            elif what[0:3] == "sin":
                nc.sync.dma_start(out=sin_sb[:, part(what[3]), :], in_=sinv[:, part(what[3]), :])
            elif len(what) > 2 and what[2] == "t":
                r, i = int(what[1]), int(what[3])
                nc.sync.dma_start(out=xtile(r)[:, i, :], in_=xv[:, r, i, :])
            elif len(what) > 2:
                r, h = int(what[1]), int(what[3])
                nc.sync.dma_start(out=xtile(r)[:, 2 * h : 2 * h + 2, :], in_=xv[:, r, 2 * h : 2 * h + 2, :])
            else:
                r = int(what[1:])
                nc.sync.dma_start(out=xtile(r)[:], in_=xv[:, r, :, :])

        def new_bank(nm):
            return psum.tile([P, 512], F32, name=nm, tag="bank")

        warm_bank = {}

        def warm(n):
            if 0 not in warm_bank:
                warm_bank[0] = new_bank("warm")
            for d in range(n):
                nc.tensor.matmul(out=warm_bank[0][:], lhsT=warm_sb[:, 0:P], rhs=warm_sb[:], start=True, stop=True)

        def copy_out(eng, dst, src):
            if eng == "S":
                nc.scalar.copy(out=dst, in_=src)
            else:
                nc.vector.tensor_copy(out=dst, in_=src)

        def quant(codes, scales, grouped2d):
            nc.vector.quantize_mx(out=codes.bitcast(FP8X4), scales=scales, in_=grouped2d)

        def mx(o, l, ls, r_, rs, start, stop):
            nc.tensor.matmul_mx(
                out=o, lhsT=l.bitcast(FP8X4), lhsT_scale=ls, rhs=r_.bitcast(FP8X4), rhs_scale=rs,
                start=start, stop=stop,
            )

        def turn(dst, words):
            nc.tensor.transpose(out=dst, in_=words, identity=ident[:])

        def turn_raw(nm, block):
            bank = new_bank(nm)
            w = block.bitcast(F32)
            for g in range(2):
                for u in range(2):
                    turn(bank[:, (2 * g + u) * P : (2 * g + u + 1) * P], w[:, 256 * g + u : 256 * (g + 1) : 2])
            return bank[:].rearrange("p (g u n) -> p g n u", g=2, u=2)

        def turn_pair(nm, blocks, g):
            n = len(blocks) * P
            bank = new_bank(nm)
            for u in range(2):
                for b in range(len(blocks)):
                    turn(bank[:, u * n + b * P : u * n + (b + 1) * P], blocks[b].bitcast(F32)[:, 256 * g + u : 256 * (g + 1) : 2])
            return bank[:, 0 : 2 * n].rearrange("p (u n) -> p n u", u=2)

        def words2(ap2d):
            return ap2d.bitcast(F32).rearrange("p (n u) -> p n u", u=2)

        def words3(ap2d):
            return ap2d.bitcast(F32).rearrange("p (g n u) -> p g n u", g=2, u=2)

        wqa_g = const.tile([P, 4, 2, P, 4], BF16, name="wqa_g", tag="wqa_g", align_bytes=64)
        wqa_c = const.tile([P, 4, 2, P], U32, name="wqa_c", tag="wqa_c", align_bytes=64)
        wqa_s = const.tile([P, 4, 2, P], U8, name="wqa_s", tag="wqa_s", align_bytes=64)
        wkv_g = const.tile([P, 2, 256, 4], BF16, name="wkv_g", tag="wkv_g", align_bytes=64)
        wkv_c = const.tile([P, 2, 256], U32, name="wkv_c", tag="wkv_c", align_bytes=64)
        wkv_s = const.tile([P, 2, 256], U8, name="wkv_s", tag="wkv_s", align_bytes=64)
        wqb_g = const.tile([P, 384, 4], BF16, name="wqb_g", tag="wqb_g", align_bytes=64)
        wqb_c = const.tile([P, 384], U32, name="wqb_c", tag="wqb_c", align_bytes=64)
        wqb_s = const.tile([P, 384], U8, name="wqb_s", tag="wqb_s", align_bytes=64)

        def wqa_t(j, eng):
            src = turn_raw("wa%d" % j, wqa_raw[:, j, :])
            copy_out(eng, words3(wqa_g[:, j, :, :, :].rearrange("p g n t -> p (g n t)")), src)

        def wqa_q(j, n=1):
            quant(
                wqa_c[:, j : j + n, :, :].rearrange("p j g n -> p (j g n)"),
                wqa_s[:, j : j + n, :, :].rearrange("p j g n -> p (j g n)"),
                wqa_g[:, j : j + n, :, :, :].rearrange("p j g n t -> p (j g n t)"),
            )

        def wkv_t(g, eng):
            src = turn_pair("wk%d" % g, [wkv_raw[:, 0, :], wkv_raw[:, 1, :]], g)
            copy_out(eng, words2(wkv_g[:, g, :, :].rearrange("p n t -> p (n t)")), src)

        def wkv_q():
            quant(
                wkv_c[:].rearrange("p g n -> p (g n)"),
                wkv_s[:].rearrange("p g n -> p (g n)"),
                wkv_g[:].rearrange("p g n t -> p (g n t)"),
            )

        def wqb_t(b, eng):
            if b == 0:
                src = turn_pair("wb0", [wqb_raw[:, 0, :], wqb_raw[:, 1, :]], 0)
                copy_out(eng, words2(wqb_g[:, 0:256, :].rearrange("p n t -> p (n t)")), src)
            else:
                src = turn_pair("wb1", [wqb_raw[:, 2, :]], 0)
                copy_out(eng, words2(wqb_g[:, 256:384, :].rearrange("p n t -> p (n t)")), src)

        def wqb_q(b):
            c = slice(0, 256) if b == 0 else slice(256, 384)
            quant(wqb_c[:, c], wqb_s[:, c], wqb_g[:, c, :].rearrange("p n t -> p (n t)"))

        def sinx(ab_):
            nc.vector.tensor_copy(out=cs[:, 1, part(ab_), 0:32], in_=sin_sb[:, part(ab_), 32:64])
            nc.vector.tensor_copy(out=cs[:, 1, part(ab_), 32:64], in_=sin_sb[:, part(ab_), 0:32])

        xd = {}
        xg = {}
        xsrc = {}
        xc = {}
        xs = {}
        qbank = {}
        qg = {}
        qc = {}
        qs = {}
        kbank = {}
        nbank = {}
        pbank = {}
        osb = {}
        tk = {}
        tq = {}

        def dx(r, i0, n):
            if r not in xd:
                xd[r] = xdp.tile([P, 2, TILES * 256, 2], BF16, name="xd%d" % r, tag="xd", align_bytes=64)
            nc.vector.tensor_copy(
                out=xd[r][:, :, i0 * 256 : (i0 + n) * 256, :],
                in_=x_sb[r][:, i0 : i0 + n, :].rearrange("p i (w u e) -> p u (i w) e", u=2, e=2),
            )

        def tx(r, i):
            if r not in xg:
                xg[r] = xgp.tile([P, TILES, 2, P, 4], BF16, name="xg%d" % r, tag="xg", align_bytes=64)
            if r in xd:
                bank = new_bank("xt%d_%d" % (r, i))
                for g in range(2):
                    for u in range(2):
                        w = xd[r][:, u, i * 256 + g * P : i * 256 + (g + 1) * P, :].rearrange("p w e -> p (w e)").bitcast(F32)
                        turn(bank[:, (2 * g + u) * P : (2 * g + u + 1) * P], w)
                xsrc[(r, i)] = bank[:].rearrange("p (g u n) -> p g n u", g=2, u=2)
            else:
                xsrc[(r, i)] = turn_raw("xt%d_%d" % (r, i), x_sb[r][:, i, :])

        def ex(r, i, eng):
            copy_out(eng, words3(xg[r][:, i, :, :, :].rearrange("p g n t -> p (g n t)")), xsrc[(r, i)])

        def vqx(r, i0, n):
            if r not in xc:
                xc[r] = xcp.tile([P, TILES, 2, P], U32, name="xc%d" % r, tag="xc", align_bytes=64)
                xs[r] = xcp.tile([P, TILES, 2, P], U8, name="xs%d" % r, tag="xs", align_bytes=64)
            t = slice(i0, i0 + n)
            quant(
                xc[r][:, t, :, :].rearrange("p i g n -> p (i g n)"),
                xs[r][:, t, :, :].rearrange("p i g n -> p (i g n)"),
                xg[r][:, t, :, :, :].rearrange("p i g n t -> p (i g n t)"),
            )

        def a(r, i):
            bank = new_bank("qa%d_%d" % (r, i))
            qbank[(r, i)] = bank
            for j in range(4):
                for g in range(2):
                    mx(
                        bank[:, j * P : (j + 1) * P],
                        wqa_c[:, j, g, :], wqa_s[:, j, g, :],
                        xc[r][:, i, g, :], xs[r][:, i, g, :],
                        g == 0, g == 1,
                    )

        def ea(r, i, eng):
            if (r, i // 2) not in qg:
                qg[(r, i // 2)] = qgp.tile([P, 2, P, 4], BF16, name="qg%d_%d" % (r, i // 2), tag="qg", align_bytes=64)
            copy_out(eng, qg[(r, i // 2)][:, i % 2, :, :], qbank[(r, i)][:].rearrange("p (j n) -> p n j", j=4))

        def vqa(r, i, n):
            pr = i // 2
            if (r, pr) not in qc:
                qc[(r, pr)] = qcp.tile([P, 2, P], U32, name="qc%d_%d" % (r, pr), tag="qc", align_bytes=64)
                qs[(r, pr)] = qcp.tile([P, 2, P], U8, name="qs%d_%d" % (r, pr), tag="qs", align_bytes=64)
            t = slice(i % 2, i % 2 + n)
            quant(
                qc[(r, pr)][:, t, :].rearrange("p i n -> p (i n)"),
                qs[(r, pr)][:, t, :].rearrange("p i n -> p (i n)"),
                qg[(r, pr)][:, t, :, :].rearrange("p i n t -> p (i n t)"),
            )

        def k(r, pr):
            bank = new_bank("kv%d_%d" % (r, pr))
            kbank[(r, pr)] = bank
            for i2 in range(2):
                for g in range(2):
                    mx(
                        bank[:, i2 * 256 : (i2 + 1) * 256],
                        xc[r][:, 2 * pr + i2, g, :], xs[r][:, 2 * pr + i2, g, :],
                        wkv_c[:, g, :], wkv_s[:, g, :],
                        g == 0, g == 1,
                    )

        def q_pass(r, i, nb, ncol, pb, pcol):
            l, ls = qc[(r, i // 2)][:, i % 2, :], qs[(r, i // 2)][:, i % 2, :]
            mx(nb[:, ncol : ncol + 256], l, ls, wqb_c[:, 0:256], wqb_s[:, 0:256], True, True)
            mx(pb[:, pcol : pcol + P], l, ls, wqb_c[:, 256:384], wqb_s[:, 256:384], True, True)

        def q(r):
            for pr in range(2):
                nbank[(r, pr)] = new_bank("qn%d_%d" % (r, pr))
                if pr == 0:
                    pbank[(r, 0)] = new_bank("qp%d" % r)
                for i2 in range(2):
                    i = 2 * pr + i2
                    q_pass(r, i, nbank[(r, pr)], i2 * 256, pbank[(r, 0)], i * P)

        def qpair(r, pr):
            nbank[(r, pr)] = new_bank("qn%d_%d" % (r, pr))
            pbank[(r, 2 * pr)] = new_bank("qp%d_%d" % (r, pr))
            for i2 in range(2):
                q_pass(r, 2 * pr + i2, nbank[(r, pr)], i2 * 256, pbank[(r, 2 * pr)], i2 * P)

        def get_o(r):
            if r not in osb:
                osb[r] = outp.tile([P, TILES, OUT_W], F32, name="o%d" % r, tag="o")
            return osb[r]

        def kv_view(r, pr):
            return kbank[(r, pr)][:].rearrange("p (i c) -> p i c", i=2)

        def vk(r, pr):
            if r not in tk:
                tk[r] = tmpp.tile([P, TILES, 2, 64], F32, name="tk%d" % r, tag="tk")
            t0 = TILES * r + 2 * pr
            nc.vector.tensor_tensor(
                out=tk[r][:, 2 * pr : 2 * pr + 2, :, :],
                in0=kv_view(r, pr)[:, :, 192:256].unsqueeze(2).to_broadcast([P, 2, 2, 64]),
                in1=cs[:, :, t0 : t0 + 2, :].rearrange("p b t c -> p t b c"),
                op=MULT,
            )

        def ek(r, pr, eng):
            copy_out(eng, get_o(r)[:, 2 * pr : 2 * pr + 2, 448:640], kv_view(r, pr)[:, :, 0:192])

        def sn(r, pr):
            o = get_o(r)[:, 2 * pr : 2 * pr + 2, 0:384].rearrange("p i (h c) -> p i h c", h=2)
            nc.scalar.copy(out=o[:, :, :, 0:128], in_=nbank[(r, pr)][:].rearrange("p (i h c) -> p i h c", i=2, h=2))

        def ab(r, i0, n):
            if r not in tq:
                tq[r] = tmpp.tile([P, 2, TILES, 2, 64], F32, name="tq%d" % r, tag="tq")
            pe = pbank[(r, i0)][:, 0 : n * P].rearrange("p (i h c) -> p i h c", i=n, h=2)
            t0 = TILES * r + i0
            for b in range(2):
                nc.vector.tensor_tensor(
                    out=tq[r][:, b, i0 : i0 + n, :, :],
                    in0=pe,
                    in1=cs[:, b, t0 : t0 + n, :].unsqueeze(2).to_broadcast([P, n, 2, 64]),
                    op=MULT,
                )

        def engine(e):
            return nc.gpsimd if e == "G" else nc.vector

        def ck(r, i0, n, e):
            o = get_o(r)
            t = tk[r]
            i = slice(i0, i0 + n)
            engine(e).tensor_tensor(out=o[:, i, 384:416], in0=t[:, i, 0, 0:32], in1=t[:, i, 1, 32:64], op=SUB)
            engine(e).tensor_tensor(out=o[:, i, 416:448], in0=t[:, i, 0, 32:64], in1=t[:, i, 1, 0:32], op=ADD)

        def cq(r, i0, n, e):
            oq = get_o(r)[:, i0 : i0 + n, 0:384].rearrange("p i (h c) -> p i h c", h=2)
            t = tq[r]
            i = slice(i0, i0 + n)
            engine(e).tensor_tensor(out=oq[:, :, :, 128:160], in0=t[:, 0, i, :, 0:32], in1=t[:, 1, i, :, 32:64], op=SUB)
            engine(e).tensor_tensor(out=oq[:, :, :, 160:192], in0=t[:, 0, i, :, 32:64], in1=t[:, 1, i, :, 0:32], op=ADD)

        def store(r, i0, n, parts):
            c0 = 0 if "q" in parts else 384
            c1 = OUT_W if "kv" in parts else 384
            nc.sync.dma_start(out=ov[:, r, i0 : i0 + n, c0:c1], in_=osb[r][:, i0 : i0 + n, c0:c1])

        load("wqa0")
        load("wqa1")
        load("wqa2")
        load("wqa3")
        load("x0t0")
        load("x0t1")
        load("x0t2")
        load("x0t3")
        load("wkv")
        load("wqb")
        load("x1")
        load("sinA")
        load("cosA")
        load("x2")
        load("x3")
        load("x4")
        load("x5")
        load("sinB")
        load("cosB")
        warm(8)
        wqa_t(0, "S")
        wqa_q(0)
        wqa_t(1, "V")
        warm(1)
        wqa_q(1)
        wqa_t(2, "S")
        wqa_q(2)
        wqa_t(3, "V")
        warm(1)
        wqa_q(3)
        tx(0, 0)
        ex(0, 0, "S")
        vqx(0, 0, 1)
        tx(0, 1)
        warm(1)
        ex(0, 1, "V")
        vqx(0, 1, 1)
        tx(0, 2)
        ex(0, 2, "S")
        vqx(0, 2, 1)
        tx(0, 3)
        warm(1)
        ex(0, 3, "V")
        vqx(0, 3, 1)
        wkv_t(0, "S")
        wkv_t(1, "V")
        warm(1)
        wqb_t(0, "S")
        wqb_t(1, "V")
        warm(1)
        wkv_q()
        wqb_q(0)
        wqb_q(1)
        a(0, 0)
        ea(0, 0, "S")
        vqa(0, 0, 1)
        a(0, 1)
        ea(0, 1, "S")
        vqa(0, 1, 1)
        a(0, 2)
        ea(0, 2, "S")
        vqa(0, 2, 1)
        sinx("A")
        a(0, 3)
        ea(0, 3, "S")
        vqa(0, 3, 1)
        tx(1, 0)
        ex(1, 0, "S")
        tx(1, 1)
        ex(1, 1, "S")
        tx(1, 2)
        ex(1, 2, "S")
        tx(1, 3)
        ex(1, 3, "S")
        k(0, 0)
        k(0, 1)
        vk(0, 0)
        ek(0, 0, "V")
        vqx(1, 0, 2)
        load("x6")
        vk(0, 1)
        ek(0, 1, "V")
        vqx(1, 2, 2)
        dx(3, 0, 4)
        tx(2, 0)
        ex(2, 0, "S")
        tx(2, 1)
        ex(2, 1, "S")
        tx(2, 2)
        ex(2, 2, "S")
        tx(2, 3)
        ex(2, 3, "S")
        q(0)
        sn(0, 0)
        sn(0, 1)
        k(1, 0)
        a(1, 0)
        k(1, 1)
        ab(0, 0, 4)
        vk(1, 0)
        ek(1, 0, "V")
        ck(0, 0, 4, "G")
        cq(0, 0, 4, "G")
        vk(1, 1)
        ek(1, 1, "V")
        store(0, 0, 4, ["q", "kv"])
        ea(1, 0, "S")
        a(1, 1)
        ea(1, 1, "S")
        vqa(1, 0, 2)
        vqx(2, 0, 2)
        a(1, 2)
        ea(1, 2, "S")
        a(1, 3)
        ea(1, 3, "S")
        vqa(1, 2, 2)
        load("x7")
        sinx("B")
        vqx(2, 2, 2)
        dx(4, 0, 4)
        tx(3, 0)
        ex(3, 0, "S")
        tx(3, 1)
        ex(3, 1, "S")
        tx(3, 2)
        ex(3, 2, "S")
        tx(3, 3)
        ex(3, 3, "S")
        q(1)
        sn(1, 0)
        sn(1, 1)
        k(2, 0)
        a(2, 0)
        k(2, 1)
        ab(1, 0, 4)
        vk(2, 0)
        ek(2, 0, "V")
        ck(1, 0, 4, "G")
        cq(1, 0, 4, "G")
        vk(2, 1)
        ek(2, 1, "V")
        store(1, 0, 4, ["q", "kv"])
        ea(2, 0, "S")
        a(2, 1)
        ea(2, 1, "S")
        vqa(2, 0, 2)
        vqx(3, 0, 2)
        a(2, 2)
        ea(2, 2, "S")
        a(2, 3)
        ea(2, 3, "S")
        vqa(2, 2, 2)
        vqx(3, 2, 2)
        dx(5, 0, 4)
        tx(4, 0)
        ex(4, 0, "S")
        tx(4, 1)
        ex(4, 1, "S")
        tx(4, 2)
        ex(4, 2, "S")
        tx(4, 3)
        ex(4, 3, "S")
        q(2)
        sn(2, 0)
        sn(2, 1)
        k(3, 0)
        a(3, 0)
        k(3, 1)
        ab(2, 0, 4)
        vk(3, 0)
        ek(3, 0, "V")
        ck(2, 0, 4, "G")
        cq(2, 0, 4, "G")
        vk(3, 1)
        ek(3, 1, "V")
        store(2, 0, 4, ["q", "kv"])
        ea(3, 0, "S")
        a(3, 1)
        ea(3, 1, "S")
        vqa(3, 0, 2)
        vqx(4, 0, 2)
        a(3, 2)
        ea(3, 2, "S")
        a(3, 3)
        ea(3, 3, "S")
        vqa(3, 2, 2)
        vqx(4, 2, 2)
        dx(6, 0, 4)
        tx(5, 0)
        ex(5, 0, "S")
        tx(5, 1)
        ex(5, 1, "S")
        tx(5, 2)
        ex(5, 2, "S")
        tx(5, 3)
        ex(5, 3, "S")
        q(3)
        sn(3, 0)
        sn(3, 1)
        k(4, 0)
        a(4, 0)
        k(4, 1)
        ab(3, 0, 4)
        vk(4, 0)
        ek(4, 0, "V")
        ck(3, 0, 4, "G")
        cq(3, 0, 4, "G")
        vk(4, 1)
        ek(4, 1, "V")
        store(3, 0, 4, ["q", "kv"])
        ea(4, 0, "S")
        a(4, 1)
        ea(4, 1, "S")
        vqa(4, 0, 2)
        vqx(5, 0, 2)
        a(4, 2)
        ea(4, 2, "S")
        a(4, 3)
        ea(4, 3, "S")
        vqa(4, 2, 2)
        vqx(5, 2, 2)
        dx(7, 0, 4)
        tx(6, 0)
        ex(6, 0, "S")
        tx(6, 1)
        ex(6, 1, "S")
        tx(6, 2)
        ex(6, 2, "S")
        tx(6, 3)
        ex(6, 3, "S")
        q(4)
        sn(4, 0)
        sn(4, 1)
        k(5, 0)
        a(5, 0)
        k(5, 1)
        ab(4, 0, 4)
        vk(5, 0)
        ek(5, 0, "V")
        ck(4, 0, 4, "G")
        cq(4, 0, 4, "G")
        vk(5, 1)
        ek(5, 1, "V")
        store(4, 0, 4, ["q", "kv"])
        ea(5, 0, "S")
        a(5, 1)
        ea(5, 1, "S")
        vqa(5, 0, 2)
        vqx(6, 0, 2)
        a(5, 2)
        ea(5, 2, "S")
        a(5, 3)
        ea(5, 3, "S")
        vqa(5, 2, 2)
        vqx(6, 2, 2)
        tx(7, 0)
        ex(7, 0, "S")
        tx(7, 1)
        ex(7, 1, "S")
        tx(7, 2)
        ex(7, 2, "S")
        tx(7, 3)
        ex(7, 3, "S")
        q(5)
        sn(5, 0)
        sn(5, 1)
        k(6, 0)
        k(6, 1)
        vqx(7, 0, 2)
        ab(5, 0, 4)
        vk(6, 0)
        ek(6, 0, "V")
        ck(5, 0, 4, "G")
        cq(5, 0, 4, "V")
        store(5, 0, 4, ["q", "kv"])
        vqx(7, 2, 2)
        a(6, 0)
        ea(6, 0, "S")
        a(6, 1)
        ea(6, 1, "S")
        vk(6, 1)
        ek(6, 1, "V")
        vqa(6, 0, 2)
        a(6, 2)
        ea(6, 2, "S")
        a(6, 3)
        ea(6, 3, "S")
        vqa(6, 2, 2)
        k(7, 0)
        ck(6, 0, 4, "G")
        store(6, 0, 4, ["kv"])
        a(7, 0)
        ea(7, 0, "S")
        vk(7, 0)
        ek(7, 0, "V")
        k(7, 1)
        vqa(7, 0, 1)
        a(7, 1)
        ea(7, 1, "S")
        vk(7, 1)
        ek(7, 1, "V")
        qpair(6, 0)
        sn(6, 0)
        ck(7, 0, 4, "G")
        store(7, 0, 4, ["kv"])
        a(7, 2)
        ea(7, 2, "S")
        ab(6, 0, 2)
        vqa(7, 1, 1)
        cq(6, 0, 2, "G")
        store(6, 0, 2, ["q"])
        qpair(6, 1)
        a(7, 3)
        ea(7, 3, "S")
        sn(6, 1)
        ab(6, 2, 2)
        vqa(7, 2, 1)
        cq(6, 2, 2, "V")
        vqa(7, 3, 1)
        store(6, 2, 2, ["q"])
        qpair(7, 0)
        sn(7, 0)
        ab(7, 0, 2)
        cq(7, 0, 2, "V")
        store(7, 0, 2, ["q"])
        qpair(7, 1)
        sn(7, 1)
        ab(7, 2, 2)
        cq(7, 2, 2, "V")
        store(7, 2, 2, ["q"])
